import numpy as np
import ml_dtypes


def mxq(x, axis, fmt="e4m3"):
    dtype, down = {"e4m3": (ml_dtypes.float8_e4m3fn, 7), "e5m2": (ml_dtypes.float8_e5m2, 14)}[fmt]
    v = np.moveaxis(np.asarray(x, np.float32).astype(ml_dtypes.bfloat16).astype(np.float64), axis, -1)
    blocks = v.reshape(v.shape[:-1] + (-1, 32))
    amax = np.abs(blocks).max(-1, keepdims=True)
    byte = np.maximum(np.where(amax > 0, np.frexp(amax)[1] - 1 + 127, 0) - down, 1)
    scale = np.exp2(byte - 127.0)
    codes = (blocks / scale).astype(np.float32).astype(dtype).astype(np.float64)
    return np.moveaxis((codes * scale).reshape(v.shape), -1, axis)


WIDE = False


def mx_kscale(k):
    if not WIDE:
        return np.ones(k)
    levels = np.array([10, -10, 5, -5, 0])
    a = np.random.permutation(np.resize(levels, k // 512 * 4)).reshape(k // 512, 4)
    idx = np.arange(k)
    return np.exp2(a[idx // 512, idx % 128 // 32])


BF16 = ml_dtypes.bfloat16


def bf(x):
    return np.asarray(x, np.float32).astype(BF16)


def f64(x):
    return np.asarray(x).astype(np.float64)


E2M1 = np.array([0.0, 0.5, 1.0, 1.5, 2.0, 3.0, 4.0, 6.0, -0.0, -0.5, -1.0, -1.5, -2.0, -3.0, -4.0, -6.0])


def pack_weight(w, fmt):
    k, n = w.shape
    w = f64(bf(w)).reshape(k // 32, 32, n)
    amax = np.abs(w).max(1)
    if fmt == "e4m3":
        byte = np.frexp(amax)[1] - 1 + 127 - 7
    else:
        mant, ex = np.frexp(amax / 6.0)
        byte = np.where(mant > 0.5, ex, ex - 1) + 127
    byte = np.clip(np.where(amax > 0, byte, 1), 1, 254)
    scaled = (w * np.exp2(127.0 - byte)[:, None, :]).reshape(k, n).astype(np.float32)
    by_word = np.ascontiguousarray(scaled.reshape(k // 512, 128, 4, n).transpose(0, 1, 3, 2))
    if fmt == "e4m3":
        words = by_word.astype(ml_dtypes.float8_e4m3fn).view(np.uint8)
    else:
        c = by_word.astype(ml_dtypes.float4_e2m1fn).view(np.uint8) & 0xF
        words = c[..., 0::2] | (c[..., 1::2] << 4)
    return np.ascontiguousarray(words), np.ascontiguousarray(byte.astype(np.uint8).reshape(k // 512, 16, n))


def unpack_weight(words, scales, fmt):
    g, p, n, _ = words.shape
    if fmt == "e4m3":
        vals = np.ascontiguousarray(words).view(ml_dtypes.float8_e4m3fn).astype(np.float64)
    else:
        nib = np.empty((g, p, n, 4), np.uint8)
        nib[..., 0::2] = words & 0xF
        nib[..., 1::2] = words >> 4
        vals = E2M1[nib]
    vals = vals * np.repeat(np.exp2(scales.astype(np.float64) - 127.0), 8, axis=1)[..., None]
    return vals.transpose(0, 1, 3, 2).reshape(g * 512, n)

def pack4(w):
    words, scales = pack_weight(w, "e2m1")
    return words.reshape(words.shape[0], 128, -1), scales


def unpack4(words, scales):
    return unpack_weight(words.reshape(words.shape[0], 128, -1, 2), scales, "e2m1")


S, B, H, NH, HD, MAX_END = 1024, 2, 1024, 16, 64, 4096
THETA = 10000.0
HALF = HD // 2
O = NH * 2 * HD


def rope(x, cos, sin):
    xr = x.reshape(S, B, NH, HALF, 2)
    x0, x1 = xr[..., 0], xr[..., 1]
    c = cos[:, None, None, :]
    sn = sin[:, None, None, :]
    o0 = x0 * c - x1 * sn
    o1 = x0 * sn + x1 * c
    return np.stack([o0, o1], axis=-1).reshape(x.shape)


def setup_inputs():
    s = mx_kscale(H)
    freqs = 1.0 / THETA ** (np.arange(0, HD, 2) / HD)
    ang = np.outer(np.arange(S), freqs)
    hidden_states = bf(np.random.standard_normal((S, B, H)) * s)
    w_qk = np.random.standard_normal((O, H)) / np.sqrt(H) / s
    words, scales = pack4(np.ascontiguousarray(w_qk.T))
    return {"hidden_states": hidden_states,
            "w_qk_words": words,
            "w_qk_scales": scales,
            "cos": bf(np.cos(ang)),
            "sin": bf(np.sin(ang))}


def reference(hidden_states, w_qk_words, w_qk_scales, cos, sin):
    mixed = mxq(f64(hidden_states), 2, "e4m3") @ unpack4(w_qk_words, w_qk_scales)
    mixed = mixed.reshape(S, B, NH, 2 * HD)
    q, k = mixed[..., :HD], mixed[..., HD:]
    q = rope(q, f64(cos), f64(sin))
    k = rope(k, f64(cos), f64(sin))
    qb = q.transpose(1, 2, 0, 3).reshape(B * NH, S, HD)
    kb = k.transpose(1, 2, 0, 3).reshape(B * NH, S, HD)
    return qb, kb

@@ -1,0 +1,155 @@
+from contextlib import ExitStack
+
+import concourse.mybir as mybir
+from concourse.masks import make_identity
+
+F32 = mybir.dt.float32
+BF16 = mybir.dt.bfloat16
+I32 = mybir.dt.int32
+U32 = mybir.dt.uint32
+U8 = mybir.dt.uint8
+FP8X4 = mybir.dt.float8_e4m3fn_x4
+FP4X4 = mybir.dt.float4_e2m1fn_x4
+MULT = mybir.AluOpType.mult
+ADD = mybir.AluOpType.add
+
+P = 128
+S, B, H = 1024, 2, 1024
+HEADS, HEAD_DIM = 16, 64
+PAIRS = HEAD_DIM // 2
+N_OUT = HEADS * 2 * HEAD_DIM
+K_PASS = 4 * P
+PASSES = H // K_PASS
+M_PER_P = S // P
+TILES = M_PER_P * B
+N_BANK = 512
+CHUNKS = N_OUT // N_BANK
+HEADS_PER_CHUNK = N_BANK // (2 * HEAD_DIM)
+VECS = 2 * HEADS_PER_CHUNK
+M_GROUP = 4
+
+FLOPS = 2 * S * B * H * N_OUT
+
+
+def tile_repro_pa_kernel(tc, hidden_states, w_qk_words, w_qk_scales, cos, sin, out_0, out_1):
+    nc = tc.nc
+    x_dram = hidden_states.rearrange("(p m) b k -> p m (b k)", m=M_PER_P)
+    out_views = [
+        o.rearrange("(b h) (p g m) d -> b g p h (m d)", b=B, p=P, m=M_GROUP) for o in (out_0, out_1)
+    ]
+
+    with ExitStack() as ctx:
+        keep = ctx.enter_context(tc.tile_pool(name="keep", bufs=1))
+        group_pool = ctx.enter_context(tc.tile_pool(name="grouped", bufs=3))
+        prod_pool = ctx.enter_context(tc.tile_pool(name="products", bufs=3))
+        stage_pool = ctx.enter_context(tc.tile_pool(name="stage", bufs=4))
+        psum_t = ctx.enter_context(tc.psum_pool(name="psum_t", bufs=2))
+        psum_acc = ctx.enter_context(tc.psum_pool(name="psum_acc", bufs=6))
+
+        w_planes = keep.tile([P, PASSES, N_OUT], U8, align_bytes=64)
+        nc.vector.memset(w_planes[:].bitcast(I32), 0)
+        for g in range(PASSES):
+            for quad in range(4):
+                nc.sync.dma_start(
+                    out=w_planes[32 * quad : 32 * quad + 4, g, :].bitcast(I32),
+                    in_=w_qk_scales[g, 4 * quad : 4 * quad + 4, :].bitcast(I32),
+                )
+
+        x_tiles = []
+        for m in range(M_PER_P):
+            x_m = keep.tile([P, B * H], BF16, name="x%d" % m)
+            x_tiles.append(x_m)
+        nc.sync.dma_start(out=x_tiles[0][:], in_=x_dram[:, 0, :])
+
+        w_words = keep.tile([P, PASSES, 2 * N_OUT], U8, align_bytes=64)
+        for g in range(PASSES):
+            nc.sync.dma_start(out=w_words[:, g, :].bitcast(I32), in_=w_qk_words[g].bitcast(I32))
+
+        cos_sb = keep.tile([P, M_PER_P, PAIRS], BF16)
+        sin_sb = keep.tile([P, M_PER_P, PAIRS], BF16)
+        nc.sync.dma_start(out=cos_sb[:], in_=cos.rearrange("(p m) j -> p m j", m=M_PER_P))
+        nc.sync.dma_start(out=sin_sb[:], in_=sin.rearrange("(p m) j -> p m j", m=M_PER_P))
+        for m in range(1, M_PER_P):
+            nc.sync.dma_start(out=x_tiles[m][:], in_=x_dram[:, m, :])
+
+        neg_sin = keep.tile([P, M_PER_P, PAIRS], BF16)
+        nc.scalar.mul(out=neg_sin[:], in_=sin_sb[:], mul=-1.0)
+
+        ident = keep.tile([P, P], F32)
+        make_identity(nc, ident[:])
+
+        x_codes = keep.tile([P, TILES, PASSES, P], U32, align_bytes=64)
+        x_scales = keep.tile([P, TILES, PASSES, P], U8, align_bytes=64)
+
+        def quantise_token_tile(t):
+            b, m = divmod(t, M_PER_P)
+            words = x_tiles[m][:].bitcast(F32)
+            flipped = psum_t.tile([P, PASSES, 2, P], F32)
+            for g in range(PASSES):
+                for u in range(2):
+                    first = (H // 2) * b + (K_PASS // 2) * g
+                    nc.tensor.transpose(
+                        flipped[:, g, u, :], words[:, first + u : first + K_PASS // 2 : 2], ident[:]
+                    )
+            grouped = group_pool.tile([P, PASSES, P, 4], BF16, align_bytes=64)
+            nc.scalar.copy(out=grouped[:].bitcast(F32), in_=flipped[:].rearrange("p g u r -> p g r u"))
+            nc.vector.quantize_mx(
+                out=x_codes[:, t, :, :].rearrange("p g r -> p (g r)").bitcast(FP8X4),
+                scales=x_scales[:, t, :, :].rearrange("p g r -> p (g r)"),
+                in_=grouped[:].rearrange("p g r t -> p (g r t)"),
+            )
+
+        quantise_token_tile(0)
+        for c in range(CHUNKS):
+            for b in range(B):
+                for group in range(M_PER_P // M_GROUP):
+                    by_cos = prod_pool.tile([P, VECS, M_GROUP, HEAD_DIM], F32)
+                    by_sin = prod_pool.tile([P, 2, VECS, M_GROUP, PAIRS], F32)
+                    for i in range(M_GROUP):
+                        m = M_GROUP * group + i
+                        t = M_PER_P * b + m
+                        if c == 0 and t + 1 < TILES:
+                            quantise_token_tile(t + 1)
+
+                        acc = psum_acc.tile([P, N_BANK], F32)
+                        for g in range(PASSES):
+                            nc.tensor.matmul_mx(
+                                out=acc[:],
+                                lhsT=x_codes[:, t, g, :].bitcast(FP8X4),
+                                lhsT_scale=x_scales[:, t, g, :],
+                                rhs=w_words[:, g, 2 * N_BANK * c : 2 * N_BANK * (c + 1)].bitcast(FP4X4),
+                                rhs_scale=w_planes[:, g, N_BANK * c : N_BANK * (c + 1)],
+                                start=(g == 0),
+                                stop=(g == PASSES - 1),
+                            )
+
+                        x = acc[:].rearrange("p (v j e) -> p v j e", j=PAIRS, e=2)
+                        nc.vector.tensor_tensor(
+                            out=by_cos[:, :, i, :].rearrange("p v (j e) -> p v j e", e=2),
+                            in0=x,
+                            in1=cos_sb[:, m, :].unsqueeze(1).unsqueeze(3).to_broadcast([P, VECS, PAIRS, 2]),
+                            op=MULT,
+                        )
+                        nc.vector.tensor_tensor(
+                            out=by_sin[:, 0, :, i, :],
+                            in0=x[:, :, :, 1],
+                            in1=neg_sin[:, m, :].unsqueeze(1).to_broadcast([P, VECS, PAIRS]),
+                            op=MULT,
+                        )
+                        nc.vector.tensor_tensor(
+                            out=by_sin[:, 1, :, i, :],
+                            in0=x[:, :, :, 0],
+                            in1=sin_sb[:, m, :].unsqueeze(1).to_broadcast([P, VECS, PAIRS]),
+                            op=MULT,
+                        )
+
+                    rotated = stage_pool.tile([P, HEADS_PER_CHUNK, 2, M_GROUP * HEAD_DIM], F32)
+                    nc.gpsimd.tensor_tensor(
+                        out=rotated[:].rearrange("p h q (n e) -> p (h q n) e", e=2),
+                        in0=by_cos[:].rearrange("p v m (j e) -> p (v m j) e", e=2),
+                        in1=by_sin[:].rearrange("p e v m j -> p (v m j) e"),
+                        op=ADD,
+                    )
+                    heads = slice(HEADS_PER_CHUNK * c, HEADS_PER_CHUNK * (c + 1))
+                    for q in range(2):
+                        nc.sync.dma_start(out=out_views[q][b, group, :, heads, :], in_=rotated[:, :, q, :])

@@ -12,21 +12,23 @@ FP8X4 = mybir.dt.float8_e4m3fn_x4
 FP4X4 = mybir.dt.float4_e2m1fn_x4
 MULT = mybir.AluOpType.mult
 ADD = mybir.AluOpType.add
+COPY = mybir.ActivationFunctionType.Copy
 
 P = 128
 S, B, H = 1024, 2, 1024
 HEADS, HEAD_DIM = 16, 64
 PAIRS = HEAD_DIM // 2
-N_OUT = HEADS * 2 * HEAD_DIM
+VECS = 2 * HEADS
+N_OUT = VECS * HEAD_DIM
 K_PASS = 4 * P
 PASSES = H // K_PASS
 M_PER_P = S // P
-TILES = M_PER_P * B
-N_BANK = 512
-CHUNKS = N_OUT // N_BANK
-HEADS_PER_CHUNK = N_BANK // (2 * HEAD_DIM)
-VECS = 2 * HEADS_PER_CHUNK
-M_GROUP = 4
+N_GROUP = 128
+GROUPS = N_OUT // N_GROUP
+ROWS = B * VECS
+BANK_PAIRS = 4
+BANKS = PAIRS // BANK_PAIRS
+M_GROUP = 2
 
 FLOPS = 2 * S * B * H * N_OUT
 
@@ -40,18 +42,19 @@ def tile_repro_pa_kernel(tc, hidden_states, w_qk_words, w_qk_scales, cos, sin, o
 
     with ExitStack() as ctx:
         keep = ctx.enter_context(tc.tile_pool(name="keep", bufs=1))
-        group_pool = ctx.enter_context(tc.tile_pool(name="grouped", bufs=3))
-        prod_pool = ctx.enter_context(tc.tile_pool(name="products", bufs=3))
-        stage_pool = ctx.enter_context(tc.tile_pool(name="stage", bufs=4))
+        group_pool = ctx.enter_context(tc.tile_pool(name="grouped", bufs=2))
+        sin_pool = ctx.enter_context(tc.tile_pool(name="by_sin", bufs=4))
+        pair_pool = ctx.enter_context(tc.tile_pool(name="by_pair", bufs=3))
+        stage_pool = ctx.enter_context(tc.tile_pool(name="stage", bufs=2))
         psum_t = ctx.enter_context(tc.psum_pool(name="psum_t", bufs=2))
         psum_acc = ctx.enter_context(tc.psum_pool(name="psum_acc", bufs=6))
 
-        w_planes = keep.tile([P, PASSES, N_OUT], U8, align_bytes=64)
-        nc.vector.memset(w_planes[:].bitcast(I32), 0)
+        s_raw = keep.tile([P, PASSES, N_OUT], U8, align_bytes=64)
+        nc.vector.memset(s_raw[:].bitcast(I32), 0)
         for g in range(PASSES):
             for quad in range(4):
                 nc.sync.dma_start(
-                    out=w_planes[32 * quad : 32 * quad + 4, g, :].bitcast(I32),
+                    out=s_raw[32 * quad : 32 * quad + 4, g, :].bitcast(I32),
                     in_=w_qk_scales[g, 4 * quad : 4 * quad + 4, :].bitcast(I32),
                 )
 
@@ -61,9 +64,9 @@ def tile_repro_pa_kernel(tc, hidden_states, w_qk_words, w_qk_scales, cos, sin, o
             x_tiles.append(x_m)
         nc.sync.dma_start(out=x_tiles[0][:], in_=x_dram[:, 0, :])
 
-        w_words = keep.tile([P, PASSES, 2 * N_OUT], U8, align_bytes=64)
+        w_raw = keep.tile([P, PASSES, 2 * N_OUT], U8, align_bytes=64)
         for g in range(PASSES):
-            nc.sync.dma_start(out=w_words[:, g, :].bitcast(I32), in_=w_qk_words[g].bitcast(I32))
+            nc.sync.dma_start(out=w_raw[:, g, :].bitcast(I32), in_=w_qk_words[g].bitcast(I32))
 
         cos_sb = keep.tile([P, M_PER_P, PAIRS], BF16)
         sin_sb = keep.tile([P, M_PER_P, PAIRS], BF16)
@@ -72,84 +75,109 @@ def tile_repro_pa_kernel(tc, hidden_states, w_qk_words, w_qk_scales, cos, sin, o
         for m in range(1, M_PER_P):
             nc.sync.dma_start(out=x_tiles[m][:], in_=x_dram[:, m, :])
 
-        neg_sin = keep.tile([P, M_PER_P, PAIRS], BF16)
-        nc.scalar.mul(out=neg_sin[:], in_=sin_sb[:], mul=-1.0)
+        cos_f = keep.tile([P, M_PER_P, PAIRS], F32)
+        sin_f = keep.tile([P, M_PER_P, PAIRS], F32)
+        neg_sin_f = keep.tile([P, M_PER_P, PAIRS], F32)
+        nc.scalar.activation(out=sin_f[:], in_=sin_sb[:], func=COPY, scale=1.0)
+        nc.scalar.activation(out=neg_sin_f[:], in_=sin_sb[:], func=COPY, scale=-1.0)
+        nc.scalar.activation(out=cos_f[:], in_=cos_sb[:], func=COPY, scale=1.0)
 
         ident = keep.tile([P, P], F32)
         make_identity(nc, ident[:])
 
-        x_codes = keep.tile([P, TILES, PASSES, P], U32, align_bytes=64)
-        x_scales = keep.tile([P, TILES, PASSES, P], U8, align_bytes=64)
-
-        def quantise_token_tile(t):
-            b, m = divmod(t, M_PER_P)
-            words = x_tiles[m][:].bitcast(F32)
-            flipped = psum_t.tile([P, PASSES, 2, P], F32)
-            for g in range(PASSES):
-                for u in range(2):
-                    first = (H // 2) * b + (K_PASS // 2) * g
-                    nc.tensor.transpose(
-                        flipped[:, g, u, :], words[:, first + u : first + K_PASS // 2 : 2], ident[:]
-                    )
-            grouped = group_pool.tile([P, PASSES, P, 4], BF16, align_bytes=64)
-            nc.scalar.copy(out=grouped[:].bitcast(F32), in_=flipped[:].rearrange("p g u r -> p g r u"))
-            nc.vector.quantize_mx(
-                out=x_codes[:, t, :, :].rearrange("p g r -> p (g r)").bitcast(FP8X4),
-                scales=x_scales[:, t, :, :].rearrange("p g r -> p (g r)"),
-                in_=grouped[:].rearrange("p g r t -> p (g r t)"),
+        w_perm = keep.tile([P, PASSES, 2 * N_OUT], U8, align_bytes=64)
+        s_perm = keep.tile([P, PASSES, N_OUT], U8, align_bytes=64)
+        for g in range(PASSES):
+            nc.vector.tensor_copy(
+                out=s_perm[:, g, :].bitcast(I32).rearrange("p (i v) -> p i v", v=VECS),
+                in_=s_raw[:, g, :].bitcast(I32).rearrange("p (v i) -> p i v", v=VECS),
+            )
+            nc.vector.tensor_copy(
+                out=w_perm[:, g, :].bitcast(I32).rearrange("p (i v c) -> p i v c", v=VECS, c=2),
+                in_=w_raw[:, g, :].bitcast(I32).rearrange("p (v i c) -> p i v c", v=VECS, c=2),
             )
 
-        quantise_token_tile(0)
-        for c in range(CHUNKS):
-            for b in range(B):
-                for group in range(M_PER_P // M_GROUP):
-                    by_cos = prod_pool.tile([P, VECS, M_GROUP, HEAD_DIM], F32)
-                    by_sin = prod_pool.tile([P, 2, VECS, M_GROUP, PAIRS], F32)
-                    for i in range(M_GROUP):
-                        m = M_GROUP * group + i
-                        t = M_PER_P * b + m
-                        if c == 0 and t + 1 < TILES:
-                            quantise_token_tile(t + 1)
+        x_codes = keep.tile([P, M_PER_P, B, PASSES, P], U32, align_bytes=64)
+        x_scales = keep.tile([P, M_PER_P, B, PASSES, P], U8, align_bytes=64)
 
-                        acc = psum_acc.tile([P, N_BANK], F32)
+        def quantise_slot(m):
+            words = x_tiles[m][:].bitcast(F32)
+            grouped = group_pool.tile([P, B, PASSES, P, 4], BF16, align_bytes=64)
+            for b in range(B):
+                flipped = psum_t.tile([P, PASSES, 2, P], F32)
+                for g in range(PASSES):
+                    for u in range(2):
+                        first = (H // 2) * b + (K_PASS // 2) * g
+                        nc.tensor.transpose(
+                            flipped[:, g, u, :], words[:, first + u : first + K_PASS // 2 : 2], ident[:]
+                        )
+                nc.scalar.copy(
+                    out=grouped[:, b].rearrange("p g r t -> p g (r t)").bitcast(F32).rearrange("p g (r u) -> p g r u", u=2),
+                    in_=flipped[:].rearrange("p g u r -> p g r u"),
+                )
+            nc.vector.quantize_mx(
+                out=x_codes[:, m].rearrange("p b g r -> p (b g r)").bitcast(FP8X4),
+                scales=x_scales[:, m].rearrange("p b g r -> p (b g r)"),
+                in_=grouped[:].rearrange("p b g r t -> p (b g r t)"),
+            )
+
+        quantise_slot(0)
+        for m in range(M_PER_P):
+            if m + 1 < M_PER_P:
+                quantise_slot(m + 1)
+            mi = m % M_GROUP
+            if mi == 0:
+                stage = stage_pool.tile([P, ROWS, M_GROUP, HEAD_DIM], F32)
+            by_pair = pair_pool.tile([P, PAIRS, 2 * ROWS], F32)
+            for k in range(BANKS):
+                acc = psum_acc.tile([P, 2, B, N_GROUP], F32)
+                for ii in range(2):
+                    i = 2 * k + ii
+                    for b in range(B):
                         for g in range(PASSES):
                             nc.tensor.matmul_mx(
-                                out=acc[:],
-                                lhsT=x_codes[:, t, g, :].bitcast(FP8X4),
-                                lhsT_scale=x_scales[:, t, g, :],
-                                rhs=w_words[:, g, 2 * N_BANK * c : 2 * N_BANK * (c + 1)].bitcast(FP4X4),
-                                rhs_scale=w_planes[:, g, N_BANK * c : N_BANK * (c + 1)],
+                                out=acc[:, ii, b, :],
+                                lhsT=x_codes[:, m, b, g, :].bitcast(FP8X4),
+                                lhsT_scale=x_scales[:, m, b, g, :],
+                                rhs=w_perm[:, g, 2 * N_GROUP * i : 2 * N_GROUP * (i + 1)].bitcast(FP4X4),
+                                rhs_scale=s_perm[:, g, N_GROUP * i : N_GROUP * (i + 1)],
                                 start=(g == 0),
                                 stop=(g == PASSES - 1),
                             )
-
-                        x = acc[:].rearrange("p (v j e) -> p v j e", j=PAIRS, e=2)
-                        nc.vector.tensor_tensor(
-                            out=by_cos[:, :, i, :].rearrange("p v (j e) -> p v j e", e=2),
-                            in0=x,
-                            in1=cos_sb[:, m, :].unsqueeze(1).unsqueeze(3).to_broadcast([P, VECS, PAIRS, 2]),
-                            op=MULT,
-                        )
-                        nc.vector.tensor_tensor(
-                            out=by_sin[:, 0, :, i, :],
-                            in0=x[:, :, :, 1],
-                            in1=neg_sin[:, m, :].unsqueeze(1).to_broadcast([P, VECS, PAIRS]),
-                            op=MULT,
-                        )
-                        nc.vector.tensor_tensor(
-                            out=by_sin[:, 1, :, i, :],
-                            in0=x[:, :, :, 0],
-                            in1=sin_sb[:, m, :].unsqueeze(1).to_broadcast([P, VECS, PAIRS]),
-                            op=MULT,
-                        )
-
-                    rotated = stage_pool.tile([P, HEADS_PER_CHUNK, 2, M_GROUP * HEAD_DIM], F32)
-                    nc.gpsimd.tensor_tensor(
-                        out=rotated[:].rearrange("p h q (n e) -> p (h q n) e", e=2),
-                        in0=by_cos[:].rearrange("p v m (j e) -> p (v m j) e", e=2),
-                        in1=by_sin[:].rearrange("p e v m j -> p (v m j) e"),
-                        op=ADD,
+                x = acc[:].rearrange("p ii b (v c) -> p ii (b v) c", c=4)
+                by_sin = sin_pool.tile([P, BANK_PAIRS, 2, ROWS], F32)
+                for jl in range(BANK_PAIRS):
+                    ii, jj = divmod(jl, 2)
+                    j = BANK_PAIRS * k + jl
+                    nc.scalar.activation(
+                        out=by_sin[:, jl, 0, :], in_=x[:, ii, :, 2 * jj + 1], func=COPY,
+                        scale=neg_sin_f[:, m, j : j + 1],
                     )
-                    heads = slice(HEADS_PER_CHUNK * c, HEADS_PER_CHUNK * (c + 1))
+                    nc.scalar.activation(
+                        out=by_sin[:, jl, 1, :], in_=x[:, ii, :, 2 * jj], func=COPY,
+                        scale=sin_f[:, m, j : j + 1],
+                    )
+                for jl in range(BANK_PAIRS):
+                    ii, jj = divmod(jl, 2)
+                    j = BANK_PAIRS * k + jl
+                    nc.vector.scalar_tensor_tensor(
+                        out=by_pair[:, j, :].rearrange("p (w e) -> p w e", e=2),
+                        in0=x[:, ii, :, 2 * jj : 2 * jj + 2],
+                        scalar=cos_f[:, m, j : j + 1],
+                        in1=by_sin[:, jl, :, :].rearrange("p e w -> p w e"),
+                        op0=MULT,
+                        op1=ADD,
+                    )
+            nc.gpsimd.tensor_scalar(
+                out=stage[:, :, mi, :].rearrange("p w (j e) -> p w j e", e=2),
+                in0=by_pair[:].rearrange("p j (w e) -> p w j e", e=2),
+                scalar1=1.0,
+                scalar2=0.0,
+                op0=MULT,
+                op1=ADD,
+            )
+            if mi == M_GROUP - 1:
+                rows = stage[:].rearrange("p (b h q) m d -> p b h q (m d)", b=B, q=2)
+                for b in range(B):
                     for q in range(2):
-                        nc.sync.dma_start(out=out_views[q][b, group, :, heads, :], in_=rotated[:, :, q, :])
+                        nc.sync.dma_start(out=out_views[q][b, m // M_GROUP], in_=rows[:, b, :, q, :])

@@ -168,13 +168,9 @@ def tile_repro_pa_kernel(tc, hidden_states, w_qk_words, w_qk_scales, cos, sin, o
                         op0=MULT,
                         op1=ADD,
                     )
-            nc.gpsimd.tensor_scalar(
+            nc.vector.tensor_copy(
                 out=stage[:, :, mi, :].rearrange("p w (j e) -> p w j e", e=2),
-                in0=by_pair[:].rearrange("p j (w e) -> p w j e", e=2),
-                scalar1=1.0,
-                scalar2=0.0,
-                op0=MULT,
-                op1=ADD,
+                in_=by_pair[:].rearrange("p j (w e) -> p w j e", e=2),
             )
             if mi == M_GROUP - 1:
                 rows = stage[:].rearrange("p (b h q) m d -> p b h q (m d)", b=B, q=2)

@@ -28,9 +28,13 @@ GROUPS = N_OUT // N_GROUP
 ROWS = B * VECS
 BANK_PAIRS = 4
 BANKS = PAIRS // BANK_PAIRS
-M_GROUP = 2
 
 FLOPS = 2 * S * B * H * N_OUT
+
+M_GROUP = 2
+PERM_CHUNKS = ((0,16),)
+SCALAR_ROWS = 16
+LAST_PIECES = 1
 
 
 def tile_repro_pa_kernel(tc, hidden_states, w_qk_words, w_qk_scales, cos, sin, out_0, out_1):
@@ -51,51 +55,34 @@ def tile_repro_pa_kernel(tc, hidden_states, w_qk_words, w_qk_scales, cos, sin, o
 
         s_raw = keep.tile([P, PASSES, N_OUT], U8, align_bytes=64)
         nc.vector.memset(s_raw[:].bitcast(I32), 0)
+        w_raw = keep.tile([P, PASSES, 2 * N_OUT], U8, align_bytes=64)
+        x_tiles = []
+        for m in range(M_PER_P):
+            x_m = keep.tile([P, B * H], BF16, name="x%d" % m)
+            x_tiles.append(x_m)
         for g in range(PASSES):
             for quad in range(4):
                 nc.sync.dma_start(
                     out=s_raw[32 * quad : 32 * quad + 4, g, :].bitcast(I32),
                     in_=w_qk_scales[g, 4 * quad : 4 * quad + 4, :].bitcast(I32),
                 )
-
-        x_tiles = []
-        for m in range(M_PER_P):
-            x_m = keep.tile([P, B * H], BF16, name="x%d" % m)
-            x_tiles.append(x_m)
         nc.sync.dma_start(out=x_tiles[0][:], in_=x_dram[:, 0, :])
-
-        w_raw = keep.tile([P, PASSES, 2 * N_OUT], U8, align_bytes=64)
         for g in range(PASSES):
             nc.sync.dma_start(out=w_raw[:, g, :].bitcast(I32), in_=w_qk_words[g].bitcast(I32))
 
         cos_sb = keep.tile([P, M_PER_P, PAIRS], BF16)
         sin_sb = keep.tile([P, M_PER_P, PAIRS], BF16)
-        nc.sync.dma_start(out=cos_sb[:], in_=cos.rearrange("(p m) j -> p m j", m=M_PER_P))
         nc.sync.dma_start(out=sin_sb[:], in_=sin.rearrange("(p m) j -> p m j", m=M_PER_P))
+        nc.sync.dma_start(out=cos_sb[:], in_=cos.rearrange("(p m) j -> p m j", m=M_PER_P))
         for m in range(1, M_PER_P):
             nc.sync.dma_start(out=x_tiles[m][:], in_=x_dram[:, m, :])
 
         cos_f = keep.tile([P, M_PER_P, PAIRS], F32)
         sin_f = keep.tile([P, M_PER_P, PAIRS], F32)
         neg_sin_f = keep.tile([P, M_PER_P, PAIRS], F32)
-        nc.scalar.activation(out=sin_f[:], in_=sin_sb[:], func=COPY, scale=1.0)
-        nc.scalar.activation(out=neg_sin_f[:], in_=sin_sb[:], func=COPY, scale=-1.0)
-        nc.scalar.activation(out=cos_f[:], in_=cos_sb[:], func=COPY, scale=1.0)
 
         ident = keep.tile([P, P], F32)
         make_identity(nc, ident[:])
-
-        w_perm = keep.tile([P, PASSES, 2 * N_OUT], U8, align_bytes=64)
-        s_perm = keep.tile([P, PASSES, N_OUT], U8, align_bytes=64)
-        for g in range(PASSES):
-            nc.vector.tensor_copy(
-                out=s_perm[:, g, :].bitcast(I32).rearrange("p (i v) -> p i v", v=VECS),
-                in_=s_raw[:, g, :].bitcast(I32).rearrange("p (v i) -> p i v", v=VECS),
-            )
-            nc.vector.tensor_copy(
-                out=w_perm[:, g, :].bitcast(I32).rearrange("p (i v c) -> p i v c", v=VECS, c=2),
-                in_=w_raw[:, g, :].bitcast(I32).rearrange("p (v i c) -> p i v c", v=VECS, c=2),
-            )
 
         x_codes = keep.tile([P, M_PER_P, B, PASSES, P], U32, align_bytes=64)
         x_scales = keep.tile([P, M_PER_P, B, PASSES, P], U8, align_bytes=64)
@@ -122,6 +109,32 @@ def tile_repro_pa_kernel(tc, hidden_states, w_qk_words, w_qk_scales, cos, sin, o
             )
 
         quantise_slot(0)
+
+        nc.scalar.activation(out=sin_f[:], in_=sin_sb[:], func=COPY, scale=1.0)
+        nc.scalar.activation(out=neg_sin_f[:], in_=sin_sb[:], func=COPY, scale=-1.0)
+        nc.scalar.activation(out=cos_f[:], in_=cos_sb[:], func=COPY, scale=1.0)
+
+        w_perm = keep.tile([P, PASSES, 2 * N_OUT], U8, align_bytes=64)
+        s_perm = keep.tile([P, PASSES, N_OUT], U8, align_bytes=64)
+        for i0, i1 in PERM_CHUNKS:
+            for g in range(PASSES):
+                nc.vector.tensor_copy(
+                    out=s_perm[:, g, :].bitcast(I32).rearrange("p (i v) -> p i v", v=VECS)[:, i0:i1, :],
+                    in_=s_raw[:, g, :].bitcast(I32).rearrange("p (v i) -> p i v", v=VECS)[:, i0:i1, :],
+                )
+                nc.vector.tensor_copy(
+                    out=w_perm[:, g, :].bitcast(I32).rearrange("p (i v c) -> p i v c", v=VECS, c=2)[:, i0:i1],
+                    in_=w_raw[:, g, :].bitcast(I32).rearrange("p (v i c) -> p i v c", v=VECS, c=2)[:, i0:i1],
+                )
+
+        def reorder(stage, mi, by_pair, j0, j1):
+            dst = stage[:, :, mi, 2 * j0 : 2 * j1].rearrange("p w (j e) -> p w j e", e=2)
+            src = by_pair[:, j0:j1, :].rearrange("p j (w e) -> p w j e", e=2)
+            split = ROWS - SCALAR_ROWS
+            nc.vector.tensor_copy(out=dst[:, :split], in_=src[:, :split])
+            if SCALAR_ROWS:
+                nc.scalar.copy(out=dst[:, split:], in_=src[:, split:])
+
         for m in range(M_PER_P):
             if m + 1 < M_PER_P:
                 quantise_slot(m + 1)
@@ -129,6 +142,8 @@ def tile_repro_pa_kernel(tc, hidden_states, w_qk_words, w_qk_scales, cos, sin, o
             if mi == 0:
                 stage = stage_pool.tile([P, ROWS, M_GROUP, HEAD_DIM], F32)
             by_pair = pair_pool.tile([P, PAIRS, 2 * ROWS], F32)
+            pieces = LAST_PIECES if m == M_PER_P - 1 else 1
+            banks_a_piece = BANKS // pieces
             for k in range(BANKS):
                 acc = psum_acc.tile([P, 2, B, N_GROUP], F32)
                 for ii in range(2):
@@ -168,10 +183,8 @@ def tile_repro_pa_kernel(tc, hidden_states, w_qk_words, w_qk_scales, cos, sin, o
                         op0=MULT,
                         op1=ADD,
                     )
-            nc.vector.tensor_copy(
-                out=stage[:, :, mi, :].rearrange("p w (j e) -> p w j e", e=2),
-                in_=by_pair[:].rearrange("p j (w e) -> p w j e", e=2),
-            )
+                if (k + 1) % banks_a_piece == 0:
+                    reorder(stage, mi, by_pair, BANK_PAIRS * (k + 1 - banks_a_piece), BANK_PAIRS * (k + 1))
             if mi == M_GROUP - 1:
                 rows = stage[:].rearrange("p (b h q) m d -> p b h q (m d)", b=B, q=2)
                 for b in range(B):

@@ -34,7 +34,7 @@ FLOPS = 2 * S * B * H * N_OUT
 M_GROUP = 2
 PERM_CHUNKS = ((0,16),)
 SCALAR_ROWS = 16
-LAST_PIECES = 1
+LAST_PIECES = 4
 
 
 def tile_repro_pa_kernel(tc, hidden_states, w_qk_words, w_qk_scales, cos, sin, out_0, out_1):
@@ -46,8 +46,8 @@ def tile_repro_pa_kernel(tc, hidden_states, w_qk_words, w_qk_scales, cos, sin, o
 
     with ExitStack() as ctx:
         keep = ctx.enter_context(tc.tile_pool(name="keep", bufs=1))
-        group_pool = ctx.enter_context(tc.tile_pool(name="grouped", bufs=2))
-        sin_pool = ctx.enter_context(tc.tile_pool(name="by_sin", bufs=4))
+        group_pool = ctx.enter_context(tc.tile_pool(name="grouped", bufs=3))
+        sin_pool = ctx.enter_context(tc.tile_pool(name="by_sin", bufs=6))
         pair_pool = ctx.enter_context(tc.tile_pool(name="by_pair", bufs=3))
         stage_pool = ctx.enter_context(tc.tile_pool(name="stage", bufs=2))
         psum_t = ctx.enter_context(tc.psum_pool(name="psum_t", bufs=2))
@@ -89,8 +89,8 @@ def tile_repro_pa_kernel(tc, hidden_states, w_qk_words, w_qk_scales, cos, sin, o
 
         def quantise_slot(m):
             words = x_tiles[m][:].bitcast(F32)
-            grouped = group_pool.tile([P, B, PASSES, P, 4], BF16, align_bytes=64)
             for b in range(B):
+                grouped = group_pool.tile([P, PASSES, P, 4], BF16, align_bytes=64)
                 flipped = psum_t.tile([P, PASSES, 2, P], F32)
                 for g in range(PASSES):
                     for u in range(2):
@@ -98,15 +98,12 @@ def tile_repro_pa_kernel(tc, hidden_states, w_qk_words, w_qk_scales, cos, sin, o
                         nc.tensor.transpose(
                             flipped[:, g, u, :], words[:, first + u : first + K_PASS // 2 : 2], ident[:]
                         )
-                nc.scalar.copy(
-                    out=grouped[:, b].rearrange("p g r t -> p g (r t)").bitcast(F32).rearrange("p g (r u) -> p g r u", u=2),
-                    in_=flipped[:].rearrange("p g u r -> p g r u"),
+                nc.scalar.copy(out=grouped[:].bitcast(F32), in_=flipped[:].rearrange("p g u r -> p g r u"))
+                nc.vector.quantize_mx(
+                    out=x_codes[:, m, b].rearrange("p g r -> p (g r)").bitcast(FP8X4),
+                    scales=x_scales[:, m, b].rearrange("p g r -> p (g r)"),
+                    in_=grouped[:].rearrange("p g r t -> p (g r t)"),
                 )
-            nc.vector.quantize_mx(
-                out=x_codes[:, m].rearrange("p b g r -> p (b g r)").bitcast(FP8X4),
-                scales=x_scales[:, m].rearrange("p b g r -> p (b g r)"),
-                in_=grouped[:].rearrange("p b g r t -> p (b g r t)"),
-            )
 
         quantise_slot(0)
 
@@ -142,7 +139,7 @@ def tile_repro_pa_kernel(tc, hidden_states, w_qk_words, w_qk_scales, cos, sin, o
             if mi == 0:
                 stage = stage_pool.tile([P, ROWS, M_GROUP, HEAD_DIM], F32)
             by_pair = pair_pool.tile([P, PAIRS, 2 * ROWS], F32)
-            pieces = LAST_PIECES if m == M_PER_P - 1 else 1
+            pieces = LAST_PIECES
             banks_a_piece = BANKS // pieces
             for k in range(BANKS):
                 acc = psum_acc.tile([P, 2, B, N_GROUP], F32)

@@ -32,7 +32,7 @@ BANKS = PAIRS // BANK_PAIRS
 FLOPS = 2 * S * B * H * N_OUT
 
 M_GROUP = 2
-PERM_CHUNKS = ((0,16),)
+PERM_CHUNKS = ((0,4),(4,16),)
 SCALAR_ROWS = 16
 LAST_PIECES = 4
 
@@ -60,15 +60,15 @@ def tile_repro_pa_kernel(tc, hidden_states, w_qk_words, w_qk_scales, cos, sin, o
         for m in range(M_PER_P):
             x_m = keep.tile([P, B * H], BF16, name="x%d" % m)
             x_tiles.append(x_m)
+        nc.sync.dma_start(out=x_tiles[0][:], in_=x_dram[:, 0, :])
+        for g in range(PASSES):
+            nc.sync.dma_start(out=w_raw[:, g, :].bitcast(I32), in_=w_qk_words[g].bitcast(I32))
         for g in range(PASSES):
             for quad in range(4):
                 nc.sync.dma_start(
                     out=s_raw[32 * quad : 32 * quad + 4, g, :].bitcast(I32),
                     in_=w_qk_scales[g, 4 * quad : 4 * quad + 4, :].bitcast(I32),
                 )
-        nc.sync.dma_start(out=x_tiles[0][:], in_=x_dram[:, 0, :])
-        for g in range(PASSES):
-            nc.sync.dma_start(out=w_raw[:, g, :].bitcast(I32), in_=w_qk_words[g].bitcast(I32))
 
         cos_sb = keep.tile([P, M_PER_P, PAIRS], BF16)
         sin_sb = keep.tile([P, M_PER_P, PAIRS], BF16)

@@ -34,6 +34,7 @@ FLOPS = 2 * S * B * H * N_OUT
 M_GROUP = 2
 PERM_CHUNKS = ((0,4),(4,16),)
 SCALAR_ROWS = 16
+PIECES = 8
 LAST_PIECES = 4
 
 
@@ -48,7 +49,7 @@ def tile_repro_pa_kernel(tc, hidden_states, w_qk_words, w_qk_scales, cos, sin, o
         keep = ctx.enter_context(tc.tile_pool(name="keep", bufs=1))
         group_pool = ctx.enter_context(tc.tile_pool(name="grouped", bufs=3))
         sin_pool = ctx.enter_context(tc.tile_pool(name="by_sin", bufs=6))
-        pair_pool = ctx.enter_context(tc.tile_pool(name="by_pair", bufs=3))
+        pair_pool = ctx.enter_context(tc.tile_pool(name="by_pair", bufs=4))
         stage_pool = ctx.enter_context(tc.tile_pool(name="stage", bufs=2))
         psum_t = ctx.enter_context(tc.psum_pool(name="psum_t", bufs=2))
         psum_acc = ctx.enter_context(tc.psum_pool(name="psum_acc", bufs=6))
@@ -98,7 +99,10 @@ def tile_repro_pa_kernel(tc, hidden_states, w_qk_words, w_qk_scales, cos, sin, o
                         nc.tensor.transpose(
                             flipped[:, g, u, :], words[:, first + u : first + K_PASS // 2 : 2], ident[:]
                         )
-                nc.scalar.copy(out=grouped[:].bitcast(F32), in_=flipped[:].rearrange("p g u r -> p g r u"))
+                if b == 0:
+                    nc.scalar.copy(out=grouped[:].bitcast(F32), in_=flipped[:].rearrange("p g u r -> p g r u"))
+                else:
+                    nc.vector.tensor_copy(out=grouped[:].bitcast(F32), in_=flipped[:].rearrange("p g u r -> p g r u"))
                 nc.vector.quantize_mx(
                     out=x_codes[:, m, b].rearrange("p g r -> p (g r)").bitcast(FP8X4),
                     scales=x_scales[:, m, b].rearrange("p g r -> p (g r)"),
@@ -124,13 +128,22 @@ def tile_repro_pa_kernel(tc, hidden_states, w_qk_words, w_qk_scales, cos, sin, o
                     in_=w_raw[:, g, :].bitcast(I32).rearrange("p (v i c) -> p i v c", v=VECS, c=2)[:, i0:i1],
                 )
 
+        def reorder_on_gpsimd(stage, mi, by_pair, j0, j1):
+            nc.gpsimd.tensor_scalar(
+                out=stage[:, :, mi, 2 * j0 : 2 * j1].rearrange("p w (j e) -> p w j e", e=2),
+                in0=by_pair[:, j0:j1, :].rearrange("p j (w e) -> p w j e", e=2),
+                scalar1=1.0,
+                scalar2=0.0,
+                op0=MULT,
+                op1=ADD,
+            )
+
         def reorder(stage, mi, by_pair, j0, j1):
             dst = stage[:, :, mi, 2 * j0 : 2 * j1].rearrange("p w (j e) -> p w j e", e=2)
             src = by_pair[:, j0:j1, :].rearrange("p j (w e) -> p w j e", e=2)
             split = ROWS - SCALAR_ROWS
             nc.vector.tensor_copy(out=dst[:, :split], in_=src[:, :split])
-            if SCALAR_ROWS:
-                nc.scalar.copy(out=dst[:, split:], in_=src[:, split:])
+            nc.scalar.copy(out=dst[:, split:], in_=src[:, split:])
 
         for m in range(M_PER_P):
             if m + 1 < M_PER_P:
@@ -139,8 +152,8 @@ def tile_repro_pa_kernel(tc, hidden_states, w_qk_words, w_qk_scales, cos, sin, o
             if mi == 0:
                 stage = stage_pool.tile([P, ROWS, M_GROUP, HEAD_DIM], F32)
             by_pair = pair_pool.tile([P, PAIRS, 2 * ROWS], F32)
-            pieces = LAST_PIECES
-            banks_a_piece = BANKS // pieces
+            banks_a_piece = BANKS // (LAST_PIECES if m == M_PER_P - 1 else PIECES)
+            put_in_order = reorder if m == M_PER_P - 1 else reorder_on_gpsimd
             for k in range(BANKS):
                 acc = psum_acc.tile([P, 2, B, N_GROUP], F32)
                 for ii in range(2):
@@ -181,7 +194,7 @@ def tile_repro_pa_kernel(tc, hidden_states, w_qk_words, w_qk_scales, cos, sin, o
                         op1=ADD,
                     )
                 if (k + 1) % banks_a_piece == 0:
-                    reorder(stage, mi, by_pair, BANK_PAIRS * (k + 1 - banks_a_piece), BANK_PAIRS * (k + 1))
+                    put_in_order(stage, mi, by_pair, BANK_PAIRS * (k + 1 - banks_a_piece), BANK_PAIRS * (k + 1))
             if mi == M_GROUP - 1:
                 rows = stage[:].rearrange("p (b h q) m d -> p b h q (m d)", b=B, q=2)
                 for b in range(B):

@@ -33,9 +33,7 @@ FLOPS = 2 * S * B * H * N_OUT
 
 M_GROUP = 2
 PERM_CHUNKS = ((0,4),(4,16),)
-SCALAR_ROWS = 16
-PIECES = 8
-LAST_PIECES = 4
+LAST_M = M_PER_P - M_GROUP
 
 
 def tile_repro_pa_kernel(tc, hidden_states, w_qk_words, w_qk_scales, cos, sin, out_0, out_1):
@@ -50,6 +48,7 @@ def tile_repro_pa_kernel(tc, hidden_states, w_qk_words, w_qk_scales, cos, sin, o
         group_pool = ctx.enter_context(tc.tile_pool(name="grouped", bufs=3))
         sin_pool = ctx.enter_context(tc.tile_pool(name="by_sin", bufs=6))
         pair_pool = ctx.enter_context(tc.tile_pool(name="by_pair", bufs=4))
+        cos_pool = ctx.enter_context(tc.tile_pool(name="by_cos", bufs=4))
         stage_pool = ctx.enter_context(tc.tile_pool(name="stage", bufs=2))
         psum_t = ctx.enter_context(tc.psum_pool(name="psum_t", bufs=2))
         psum_acc = ctx.enter_context(tc.psum_pool(name="psum_acc", bufs=6))
@@ -81,6 +80,7 @@ def tile_repro_pa_kernel(tc, hidden_states, w_qk_words, w_qk_scales, cos, sin, o
         cos_f = keep.tile([P, M_PER_P, PAIRS], F32)
         sin_f = keep.tile([P, M_PER_P, PAIRS], F32)
         neg_sin_f = keep.tile([P, M_PER_P, PAIRS], F32)
+        signed_sin_f = keep.tile([P, M_GROUP, PAIRS, 2], F32)
 
         ident = keep.tile([P, P], F32)
         make_identity(nc, ident[:])
@@ -99,7 +99,7 @@ def tile_repro_pa_kernel(tc, hidden_states, w_qk_words, w_qk_scales, cos, sin, o
                         nc.tensor.transpose(
                             flipped[:, g, u, :], words[:, first + u : first + K_PASS // 2 : 2], ident[:]
                         )
-                if b == 0:
+                if b == 0 or m % 2 == 0:
                     nc.scalar.copy(out=grouped[:].bitcast(F32), in_=flipped[:].rearrange("p g u r -> p g r u"))
                 else:
                     nc.vector.tensor_copy(out=grouped[:].bitcast(F32), in_=flipped[:].rearrange("p g u r -> p g r u"))
@@ -114,6 +114,12 @@ def tile_repro_pa_kernel(tc, hidden_states, w_qk_words, w_qk_scales, cos, sin, o
         nc.scalar.activation(out=sin_f[:], in_=sin_sb[:], func=COPY, scale=1.0)
         nc.scalar.activation(out=neg_sin_f[:], in_=sin_sb[:], func=COPY, scale=-1.0)
         nc.scalar.activation(out=cos_f[:], in_=cos_sb[:], func=COPY, scale=1.0)
+        nc.gpsimd.tensor_scalar(
+            out=signed_sin_f[:, :, :, 0], in0=sin_sb[:, LAST_M:, :], scalar1=-1.0, scalar2=None, op0=MULT
+        )
+        nc.gpsimd.tensor_scalar(
+            out=signed_sin_f[:, :, :, 1], in0=sin_sb[:, LAST_M:, :], scalar1=1.0, scalar2=None, op0=MULT
+        )
 
         w_perm = keep.tile([P, PASSES, 2 * N_OUT], U8, align_bytes=64)
         s_perm = keep.tile([P, PASSES, N_OUT], U8, align_bytes=64)
@@ -138,38 +144,34 @@ def tile_repro_pa_kernel(tc, hidden_states, w_qk_words, w_qk_scales, cos, sin, o
                 op1=ADD,
             )
 
-        def reorder(stage, mi, by_pair, j0, j1):
-            dst = stage[:, :, mi, 2 * j0 : 2 * j1].rearrange("p w (j e) -> p w j e", e=2)
-            src = by_pair[:, j0:j1, :].rearrange("p j (w e) -> p w j e", e=2)
-            split = ROWS - SCALAR_ROWS
-            nc.vector.tensor_copy(out=dst[:, :split], in_=src[:, :split])
-            nc.scalar.copy(out=dst[:, split:], in_=src[:, split:])
+        def project(acc, m, columns_and_batches):
+            for slot, (i, b) in enumerate(columns_and_batches):
+                for g in range(PASSES):
+                    nc.tensor.matmul_mx(
+                        out=acc[:, N_GROUP * slot : N_GROUP * (slot + 1)],
+                        lhsT=x_codes[:, m, b, g, :].bitcast(FP8X4),
+                        lhsT_scale=x_scales[:, m, b, g, :],
+                        rhs=w_perm[:, g, 2 * N_GROUP * i : 2 * N_GROUP * (i + 1)].bitcast(FP4X4),
+                        rhs_scale=s_perm[:, g, N_GROUP * i : N_GROUP * (i + 1)],
+                        start=(g == 0),
+                        stop=(g == PASSES - 1),
+                    )
 
-        for m in range(M_PER_P):
-            if m + 1 < M_PER_P:
-                quantise_slot(m + 1)
+        def store(stage, m_set, b):
+            rows = stage[:].rearrange("p (b h q) m d -> p b h q (m d)", b=B, q=2)
+            for q in range(2):
+                nc.sync.dma_start(out=out_views[q][b, m_set], in_=rows[:, b, :, q, :])
+
+        for m in range(LAST_M):
+            quantise_slot(m + 1)
             mi = m % M_GROUP
             if mi == 0:
                 stage = stage_pool.tile([P, ROWS, M_GROUP, HEAD_DIM], F32)
             by_pair = pair_pool.tile([P, PAIRS, 2 * ROWS], F32)
-            banks_a_piece = BANKS // (LAST_PIECES if m == M_PER_P - 1 else PIECES)
-            put_in_order = reorder if m == M_PER_P - 1 else reorder_on_gpsimd
             for k in range(BANKS):
-                acc = psum_acc.tile([P, 2, B, N_GROUP], F32)
-                for ii in range(2):
-                    i = 2 * k + ii
-                    for b in range(B):
-                        for g in range(PASSES):
-                            nc.tensor.matmul_mx(
-                                out=acc[:, ii, b, :],
-                                lhsT=x_codes[:, m, b, g, :].bitcast(FP8X4),
-                                lhsT_scale=x_scales[:, m, b, g, :],
-                                rhs=w_perm[:, g, 2 * N_GROUP * i : 2 * N_GROUP * (i + 1)].bitcast(FP4X4),
-                                rhs_scale=s_perm[:, g, N_GROUP * i : N_GROUP * (i + 1)],
-                                start=(g == 0),
-                                stop=(g == PASSES - 1),
-                            )
-                x = acc[:].rearrange("p ii b (v c) -> p ii (b v) c", c=4)
+                acc = psum_acc.tile([P, 4 * N_GROUP], F32)
+                project(acc, m, [(2 * k + ii, b) for ii in range(2) for b in range(B)])
+                x = acc[:].rearrange("p (ii w c) -> p ii w c", ii=2, c=4)
                 by_sin = sin_pool.tile([P, BANK_PAIRS, 2, ROWS], F32)
                 for jl in range(BANK_PAIRS):
                     ii, jj = divmod(jl, 2)
@@ -193,10 +195,43 @@ def tile_repro_pa_kernel(tc, hidden_states, w_qk_words, w_qk_scales, cos, sin, o
                         op0=MULT,
                         op1=ADD,
                     )
-                if (k + 1) % banks_a_piece == 0:
-                    put_in_order(stage, mi, by_pair, BANK_PAIRS * (k + 1 - banks_a_piece), BANK_PAIRS * (k + 1))
+                reorder_on_gpsimd(stage, mi, by_pair, BANK_PAIRS * k, BANK_PAIRS * (k + 1))
             if mi == M_GROUP - 1:
-                rows = stage[:].rearrange("p (b h q) m d -> p b h q (m d)", b=B, q=2)
                 for b in range(B):
-                    for q in range(2):
-                        nc.sync.dma_start(out=out_views[q][b, m // M_GROUP], in_=rows[:, b, :, q, :])
+                    store(stage, m // M_GROUP, b)
+
+        quantise_slot(M_PER_P - 1)
+        stage = stage_pool.tile([P, ROWS, M_GROUP, HEAD_DIM], F32)
+        for b in range(B):
+            for mi in range(M_GROUP):
+                m = LAST_M + mi
+                for k in range(BANKS // B):
+                    acc = psum_acc.tile([P, 4 * N_GROUP], F32)
+                    project(acc, m, [(4 * k + ii, b) for ii in range(4)])
+                    x = acc[:].rearrange("p (ii v c) -> p ii v c", ii=4, c=4)
+                    j0 = B * BANK_PAIRS * k
+                    by_cos = cos_pool.tile([P, B * BANK_PAIRS, 2 * VECS], F32)
+                    for jl in range(B * BANK_PAIRS):
+                        ii, jj = divmod(jl, 2)
+                        nc.scalar.activation(
+                            out=by_cos[:, jl, :].rearrange("p (v e) -> p v e", e=2),
+                            in_=x[:, ii, :, 2 * jj : 2 * jj + 2],
+                            func=COPY,
+                            scale=cos_f[:, m, j0 + jl : j0 + jl + 1],
+                        )
+                    rows = stage[:, VECS * b : VECS * (b + 1), mi, 2 * j0 : 2 * (j0 + B * BANK_PAIRS)]
+                    nc.vector.tensor_tensor(
+                        out=rows.rearrange("p v (ii jj e) -> p ii v jj e", ii=4, jj=2),
+                        in0=x.rearrange("p ii v (jj e) -> p ii v jj e", jj=2)[:, :, :, :, ::-1],
+                        in1=signed_sin_f[:, mi, j0 : j0 + B * BANK_PAIRS, :]
+                        .rearrange("p (ii jj) e -> p ii jj e", ii=4)
+                        .unsqueeze(2)
+                        .to_broadcast([P, 4, VECS, 2, 2]),
+                        op=MULT,
+                    )
+                    sums = rows.rearrange("p v (j e) -> p v j e", e=2)
+                    adder = nc.gpsimd if b == 0 and k % 2 == 0 else nc.vector
+                    adder.tensor_tensor(
+                        out=sums, in0=sums, in1=by_cos[:].rearrange("p j (v e) -> p v j e", e=2), op=ADD
+                    )
+            store(stage, LAST_M // M_GROUP, b)

@@ -47,7 +47,7 @@ def tile_repro_pa_kernel(tc, hidden_states, w_qk_words, w_qk_scales, cos, sin, o
         keep = ctx.enter_context(tc.tile_pool(name="keep", bufs=1))
         group_pool = ctx.enter_context(tc.tile_pool(name="grouped", bufs=3))
         sin_pool = ctx.enter_context(tc.tile_pool(name="by_sin", bufs=6))
-        pair_pool = ctx.enter_context(tc.tile_pool(name="by_pair", bufs=4))
+        pair_pool = ctx.enter_context(tc.tile_pool(name="by_pair", bufs=12))
         cos_pool = ctx.enter_context(tc.tile_pool(name="by_cos", bufs=4))
         stage_pool = ctx.enter_context(tc.tile_pool(name="stage", bufs=2))
         psum_t = ctx.enter_context(tc.psum_pool(name="psum_t", bufs=2))
@@ -90,8 +90,8 @@ def tile_repro_pa_kernel(tc, hidden_states, w_qk_words, w_qk_scales, cos, sin, o
 
         def quantise_slot(m):
             words = x_tiles[m][:].bitcast(F32)
+            grouped = group_pool.tile([P, B, PASSES, P, 4], BF16, align_bytes=64)
             for b in range(B):
-                grouped = group_pool.tile([P, PASSES, P, 4], BF16, align_bytes=64)
                 flipped = psum_t.tile([P, PASSES, 2, P], F32)
                 for g in range(PASSES):
                     for u in range(2):
@@ -99,15 +99,16 @@ def tile_repro_pa_kernel(tc, hidden_states, w_qk_words, w_qk_scales, cos, sin, o
                         nc.tensor.transpose(
                             flipped[:, g, u, :], words[:, first + u : first + K_PASS // 2 : 2], ident[:]
                         )
+                half = grouped[:, b].bitcast(F32)
                 if b == 0 or m % 2 == 0:
-                    nc.scalar.copy(out=grouped[:].bitcast(F32), in_=flipped[:].rearrange("p g u r -> p g r u"))
+                    nc.scalar.copy(out=half, in_=flipped[:].rearrange("p g u r -> p g r u"))
                 else:
-                    nc.vector.tensor_copy(out=grouped[:].bitcast(F32), in_=flipped[:].rearrange("p g u r -> p g r u"))
-                nc.vector.quantize_mx(
-                    out=x_codes[:, m, b].rearrange("p g r -> p (g r)").bitcast(FP8X4),
-                    scales=x_scales[:, m, b].rearrange("p g r -> p (g r)"),
-                    in_=grouped[:].rearrange("p g r t -> p (g r t)"),
-                )
+                    nc.vector.tensor_copy(out=half, in_=flipped[:].rearrange("p g u r -> p g r u"))
+            nc.vector.quantize_mx(
+                out=x_codes[:, m].rearrange("p b g r -> p (b g r)").bitcast(FP8X4),
+                scales=x_scales[:, m].rearrange("p b g r -> p (b g r)"),
+                in_=grouped[:].rearrange("p b g r t -> p (b g r t)"),
+            )
 
         quantise_slot(0)
 
@@ -137,7 +138,7 @@ def tile_repro_pa_kernel(tc, hidden_states, w_qk_words, w_qk_scales, cos, sin, o
         def reorder_on_gpsimd(stage, mi, by_pair, j0, j1):
             nc.gpsimd.tensor_scalar(
                 out=stage[:, :, mi, 2 * j0 : 2 * j1].rearrange("p w (j e) -> p w j e", e=2),
-                in0=by_pair[:, j0:j1, :].rearrange("p j (w e) -> p w j e", e=2),
+                in0=by_pair[:].rearrange("p j (w e) -> p w j e", e=2),
                 scalar1=1.0,
                 scalar2=0.0,
                 op0=MULT,
@@ -167,12 +168,12 @@ def tile_repro_pa_kernel(tc, hidden_states, w_qk_words, w_qk_scales, cos, sin, o
             mi = m % M_GROUP
             if mi == 0:
                 stage = stage_pool.tile([P, ROWS, M_GROUP, HEAD_DIM], F32)
-            by_pair = pair_pool.tile([P, PAIRS, 2 * ROWS], F32)
             for k in range(BANKS):
                 acc = psum_acc.tile([P, 4 * N_GROUP], F32)
                 project(acc, m, [(2 * k + ii, b) for ii in range(2) for b in range(B)])
                 x = acc[:].rearrange("p (ii w c) -> p ii w c", ii=2, c=4)
                 by_sin = sin_pool.tile([P, BANK_PAIRS, 2, ROWS], F32)
+                by_pair = pair_pool.tile([P, BANK_PAIRS, 2 * ROWS], F32)
                 for jl in range(BANK_PAIRS):
                     ii, jj = divmod(jl, 2)
                     j = BANK_PAIRS * k + jl
@@ -188,7 +189,7 @@ def tile_repro_pa_kernel(tc, hidden_states, w_qk_words, w_qk_scales, cos, sin, o
                     ii, jj = divmod(jl, 2)
                     j = BANK_PAIRS * k + jl
                     nc.vector.scalar_tensor_tensor(
-                        out=by_pair[:, j, :].rearrange("p (w e) -> p w e", e=2),
+                        out=by_pair[:, jl, :].rearrange("p (w e) -> p w e", e=2),
                         in0=x[:, ii, :, 2 * jj : 2 * jj + 2],
                         scalar=cos_f[:, m, j : j + 1],
                         in1=by_sin[:, jl, :, :].rearrange("p e w -> p w e"),

@@ -33,7 +33,7 @@ FLOPS = 2 * S * B * H * N_OUT
 
 M_GROUP = 2
 PERM_CHUNKS = ((0,4),(4,16),)
-LAST_M = M_PER_P - M_GROUP
+SPLIT_FROM = 5
 
 
 def tile_repro_pa_kernel(tc, hidden_states, w_qk_words, w_qk_scales, cos, sin, out_0, out_1):
@@ -80,7 +80,7 @@ def tile_repro_pa_kernel(tc, hidden_states, w_qk_words, w_qk_scales, cos, sin, o
         cos_f = keep.tile([P, M_PER_P, PAIRS], F32)
         sin_f = keep.tile([P, M_PER_P, PAIRS], F32)
         neg_sin_f = keep.tile([P, M_PER_P, PAIRS], F32)
-        signed_sin_f = keep.tile([P, M_GROUP, PAIRS, 2], F32)
+        signed_sin_f = keep.tile([P, len(range(SPLIT_FROM, M_PER_P, 2)), PAIRS, 2], F32)
 
         ident = keep.tile([P, P], F32)
         make_identity(nc, ident[:])
@@ -116,10 +116,10 @@ def tile_repro_pa_kernel(tc, hidden_states, w_qk_words, w_qk_scales, cos, sin, o
         nc.scalar.activation(out=neg_sin_f[:], in_=sin_sb[:], func=COPY, scale=-1.0)
         nc.scalar.activation(out=cos_f[:], in_=cos_sb[:], func=COPY, scale=1.0)
         nc.gpsimd.tensor_scalar(
-            out=signed_sin_f[:, :, :, 0], in0=sin_sb[:, LAST_M:, :], scalar1=-1.0, scalar2=None, op0=MULT
+            out=signed_sin_f[:, :, :, 0], in0=sin_sb[:, SPLIT_FROM::2, :], scalar1=-1.0, scalar2=None, op0=MULT
         )
         nc.gpsimd.tensor_scalar(
-            out=signed_sin_f[:, :, :, 1], in0=sin_sb[:, LAST_M:, :], scalar1=1.0, scalar2=None, op0=MULT
+            out=signed_sin_f[:, :, :, 1], in0=sin_sb[:, SPLIT_FROM::2, :], scalar1=1.0, scalar2=None, op0=MULT
         )
 
         w_perm = keep.tile([P, PASSES, 2 * N_OUT], U8, align_bytes=64)
@@ -145,32 +145,31 @@ def tile_repro_pa_kernel(tc, hidden_states, w_qk_words, w_qk_scales, cos, sin, o
                 op1=ADD,
             )
 
-        def project(acc, m, columns_and_batches):
-            for slot, (i, b) in enumerate(columns_and_batches):
-                for g in range(PASSES):
-                    nc.tensor.matmul_mx(
-                        out=acc[:, N_GROUP * slot : N_GROUP * (slot + 1)],
-                        lhsT=x_codes[:, m, b, g, :].bitcast(FP8X4),
-                        lhsT_scale=x_scales[:, m, b, g, :],
-                        rhs=w_perm[:, g, 2 * N_GROUP * i : 2 * N_GROUP * (i + 1)].bitcast(FP4X4),
-                        rhs_scale=s_perm[:, g, N_GROUP * i : N_GROUP * (i + 1)],
-                        start=(g == 0),
-                        stop=(g == PASSES - 1),
-                    )
+        def project(out, m, b, first, width):
+            for g in range(PASSES):
+                nc.tensor.matmul_mx(
+                    out=out,
+                    lhsT=x_codes[:, m, b, g, :].bitcast(FP8X4),
+                    lhsT_scale=x_scales[:, m, b, g, :],
+                    rhs=w_perm[:, g, 2 * first : 2 * (first + width)].bitcast(FP4X4),
+                    rhs_scale=s_perm[:, g, first : first + width],
+                    start=(g == 0),
+                    stop=(g == PASSES - 1),
+                )
 
         def store(stage, m_set, b):
             rows = stage[:].rearrange("p (b h q) m d -> p b h q (m d)", b=B, q=2)
             for q in range(2):
                 nc.sync.dma_start(out=out_views[q][b, m_set], in_=rows[:, b, :, q, :])
 
-        for m in range(LAST_M):
-            quantise_slot(m + 1)
+        def both_batches(m, stage):
             mi = m % M_GROUP
-            if mi == 0:
-                stage = stage_pool.tile([P, ROWS, M_GROUP, HEAD_DIM], F32)
             for k in range(BANKS):
                 acc = psum_acc.tile([P, 4 * N_GROUP], F32)
-                project(acc, m, [(2 * k + ii, b) for ii in range(2) for b in range(B)])
+                for ii in range(2):
+                    for b in range(B):
+                        part = N_GROUP * (B * ii + b)
+                        project(acc[:, part : part + N_GROUP], m, b, N_GROUP * (2 * k + ii), N_GROUP)
                 x = acc[:].rearrange("p (ii w c) -> p ii w c", ii=2, c=4)
                 by_sin = sin_pool.tile([P, BANK_PAIRS, 2, ROWS], F32)
                 by_pair = pair_pool.tile([P, BANK_PAIRS, 2 * ROWS], F32)
@@ -197,42 +196,50 @@ def tile_repro_pa_kernel(tc, hidden_states, w_qk_words, w_qk_scales, cos, sin, o
                         op1=ADD,
                     )
                 reorder_on_gpsimd(stage, mi, by_pair, BANK_PAIRS * k, BANK_PAIRS * (k + 1))
-            if mi == M_GROUP - 1:
-                for b in range(B):
-                    store(stage, m // M_GROUP, b)
 
-        quantise_slot(M_PER_P - 1)
-        stage = stage_pool.tile([P, ROWS, M_GROUP, HEAD_DIM], F32)
-        for b in range(B):
-            for mi in range(M_GROUP):
-                m = LAST_M + mi
-                for k in range(BANKS // B):
-                    acc = psum_acc.tile([P, 4 * N_GROUP], F32)
-                    project(acc, m, [(4 * k + ii, b) for ii in range(4)])
-                    x = acc[:].rearrange("p (ii v c) -> p ii v c", ii=4, c=4)
-                    j0 = B * BANK_PAIRS * k
-                    by_cos = cos_pool.tile([P, B * BANK_PAIRS, 2 * VECS], F32)
-                    for jl in range(B * BANK_PAIRS):
-                        ii, jj = divmod(jl, 2)
-                        nc.scalar.activation(
-                            out=by_cos[:, jl, :].rearrange("p (v e) -> p v e", e=2),
-                            in_=x[:, ii, :, 2 * jj : 2 * jj + 2],
-                            func=COPY,
-                            scale=cos_f[:, m, j0 + jl : j0 + jl + 1],
-                        )
-                    rows = stage[:, VECS * b : VECS * (b + 1), mi, 2 * j0 : 2 * (j0 + B * BANK_PAIRS)]
-                    nc.vector.tensor_tensor(
-                        out=rows.rearrange("p v (ii jj e) -> p ii v jj e", ii=4, jj=2),
-                        in0=x.rearrange("p ii v (jj e) -> p ii v jj e", jj=2)[:, :, :, :, ::-1],
-                        in1=signed_sin_f[:, mi, j0 : j0 + B * BANK_PAIRS, :]
-                        .rearrange("p (ii jj) e -> p ii jj e", ii=4)
-                        .unsqueeze(2)
-                        .to_broadcast([P, 4, VECS, 2, 2]),
-                        op=MULT,
+        def one_batch(m, b, stage):
+            mi = m % M_GROUP
+            for k in range(BANKS // B):
+                acc = psum_acc.tile([P, 4 * N_GROUP], F32)
+                project(acc[:], m, b, 4 * N_GROUP * k, 4 * N_GROUP)
+                x = acc[:].rearrange("p (ii v c) -> p ii v c", ii=4, c=4)
+                j0 = B * BANK_PAIRS * k
+                by_cos = cos_pool.tile([P, B * BANK_PAIRS, 2 * VECS], F32)
+                for jl in range(B * BANK_PAIRS):
+                    ii, jj = divmod(jl, 2)
+                    nc.scalar.activation(
+                        out=by_cos[:, jl, :].rearrange("p (v e) -> p v e", e=2),
+                        in_=x[:, ii, :, 2 * jj : 2 * jj + 2],
+                        func=COPY,
+                        scale=cos_f[:, m, j0 + jl : j0 + jl + 1],
                     )
-                    sums = rows.rearrange("p v (j e) -> p v j e", e=2)
-                    adder = nc.gpsimd if b == 0 and k % 2 == 0 else nc.vector
-                    adder.tensor_tensor(
-                        out=sums, in0=sums, in1=by_cos[:].rearrange("p j (v e) -> p v j e", e=2), op=ADD
-                    )
-            store(stage, LAST_M // M_GROUP, b)
+                rows = stage[:, VECS * b : VECS * (b + 1), mi, 2 * j0 : 2 * (j0 + B * BANK_PAIRS)]
+                nc.vector.tensor_tensor(
+                    out=rows.rearrange("p v (ii jj e) -> p ii v jj e", ii=4, jj=2),
+                    in0=x.rearrange("p ii v (jj e) -> p ii v jj e", jj=2)[:, :, :, :, ::-1],
+                    in1=signed_sin_f[:, (m - SPLIT_FROM) // 2, j0 : j0 + B * BANK_PAIRS, :]
+                    .rearrange("p (ii jj) e -> p ii jj e", ii=4)
+                    .unsqueeze(2)
+                    .to_broadcast([P, 4, VECS, 2, 2]),
+                    op=MULT,
+                )
+                sums = rows.rearrange("p v (j e) -> p v j e", e=2)
+                last_half = m == M_PER_P - 1 and b == B - 1
+                adder = nc.gpsimd if k % 2 == 0 and not last_half else nc.vector
+                adder.tensor_tensor(
+                    out=sums, in0=sums, in1=by_cos[:].rearrange("p j (v e) -> p v j e", e=2), op=ADD
+                )
+
+        for m in range(M_PER_P):
+            if m + 1 < M_PER_P:
+                quantise_slot(m + 1)
+            if m % M_GROUP == 0:
+                stage = stage_pool.tile([P, ROWS, M_GROUP, HEAD_DIM], F32)
+            split = m >= SPLIT_FROM and (m - SPLIT_FROM) % 2 == 0
+            if not split:
+                both_batches(m, stage)
+            for b in range(B):
+                if split:
+                    one_batch(m, b, stage)
+                if m % M_GROUP == M_GROUP - 1:
+                    store(stage, m // M_GROUP, b)

@@ -33,7 +33,8 @@ FLOPS = 2 * S * B * H * N_OUT
 
 M_GROUP = 2
 PERM_CHUNKS = ((0,4),(4,16),)
-SPLIT_FROM = 5
+GPSIMD_BANKS = (0, 2, 3, 5, 7)
+SCALAR_BANKS = (1, 4)
 
 
 def tile_repro_pa_kernel(tc, hidden_states, w_qk_words, w_qk_scales, cos, sin, out_0, out_1):
@@ -47,8 +48,8 @@ def tile_repro_pa_kernel(tc, hidden_states, w_qk_words, w_qk_scales, cos, sin, o
         keep = ctx.enter_context(tc.tile_pool(name="keep", bufs=1))
         group_pool = ctx.enter_context(tc.tile_pool(name="grouped", bufs=3))
         sin_pool = ctx.enter_context(tc.tile_pool(name="by_sin", bufs=6))
-        pair_pool = ctx.enter_context(tc.tile_pool(name="by_pair", bufs=12))
-        cos_pool = ctx.enter_context(tc.tile_pool(name="by_cos", bufs=4))
+        pair_pool = ctx.enter_context(tc.tile_pool(name="by_pair", bufs=4))
+        cos_pool = ctx.enter_context(tc.tile_pool(name="by_cos", bufs=8))
         stage_pool = ctx.enter_context(tc.tile_pool(name="stage", bufs=2))
         psum_t = ctx.enter_context(tc.psum_pool(name="psum_t", bufs=2))
         psum_acc = ctx.enter_context(tc.psum_pool(name="psum_acc", bufs=6))
@@ -61,6 +62,10 @@ def tile_repro_pa_kernel(tc, hidden_states, w_qk_words, w_qk_scales, cos, sin, o
             x_m = keep.tile([P, B * H], BF16, name="x%d" % m)
             x_tiles.append(x_m)
         nc.sync.dma_start(out=x_tiles[0][:], in_=x_dram[:, 0, :])
+        cos_sb = keep.tile([P, M_PER_P, PAIRS], BF16)
+        sin_sb = keep.tile([P, M_PER_P, PAIRS], BF16)
+        nc.sync.dma_start(out=sin_sb[:], in_=sin.rearrange("(p m) j -> p m j", m=M_PER_P))
+        nc.sync.dma_start(out=cos_sb[:], in_=cos.rearrange("(p m) j -> p m j", m=M_PER_P))
         for g in range(PASSES):
             nc.sync.dma_start(out=w_raw[:, g, :].bitcast(I32), in_=w_qk_words[g].bitcast(I32))
         for g in range(PASSES):
@@ -70,17 +75,11 @@ def tile_repro_pa_kernel(tc, hidden_states, w_qk_words, w_qk_scales, cos, sin, o
                     in_=w_qk_scales[g, 4 * quad : 4 * quad + 4, :].bitcast(I32),
                 )
 
-        cos_sb = keep.tile([P, M_PER_P, PAIRS], BF16)
-        sin_sb = keep.tile([P, M_PER_P, PAIRS], BF16)
-        nc.sync.dma_start(out=sin_sb[:], in_=sin.rearrange("(p m) j -> p m j", m=M_PER_P))
-        nc.sync.dma_start(out=cos_sb[:], in_=cos.rearrange("(p m) j -> p m j", m=M_PER_P))
         for m in range(1, M_PER_P):
             nc.sync.dma_start(out=x_tiles[m][:], in_=x_dram[:, m, :])
 
         cos_f = keep.tile([P, M_PER_P, PAIRS], F32)
-        sin_f = keep.tile([P, M_PER_P, PAIRS], F32)
-        neg_sin_f = keep.tile([P, M_PER_P, PAIRS], F32)
-        signed_sin_f = keep.tile([P, len(range(SPLIT_FROM, M_PER_P, 2)), PAIRS, 2], F32)
+        signed_sin_f = keep.tile([P, M_PER_P, PAIRS, 2], F32)
 
         ident = keep.tile([P, P], F32)
         make_identity(nc, ident[:])
@@ -100,7 +99,7 @@ def tile_repro_pa_kernel(tc, hidden_states, w_qk_words, w_qk_scales, cos, sin, o
                             flipped[:, g, u, :], words[:, first + u : first + K_PASS // 2 : 2], ident[:]
                         )
                 half = grouped[:, b].bitcast(F32)
-                if b == 0 or m % 2 == 0:
+                if b == 0:
                     nc.scalar.copy(out=half, in_=flipped[:].rearrange("p g u r -> p g r u"))
                 else:
                     nc.vector.tensor_copy(out=half, in_=flipped[:].rearrange("p g u r -> p g r u"))
@@ -112,15 +111,11 @@ def tile_repro_pa_kernel(tc, hidden_states, w_qk_words, w_qk_scales, cos, sin, o
 
         quantise_slot(0)
 
-        nc.scalar.activation(out=sin_f[:], in_=sin_sb[:], func=COPY, scale=1.0)
-        nc.scalar.activation(out=neg_sin_f[:], in_=sin_sb[:], func=COPY, scale=-1.0)
-        nc.scalar.activation(out=cos_f[:], in_=cos_sb[:], func=COPY, scale=1.0)
-        nc.gpsimd.tensor_scalar(
-            out=signed_sin_f[:, :, :, 0], in0=sin_sb[:, SPLIT_FROM::2, :], scalar1=-1.0, scalar2=None, op0=MULT
-        )
-        nc.gpsimd.tensor_scalar(
-            out=signed_sin_f[:, :, :, 1], in0=sin_sb[:, SPLIT_FROM::2, :], scalar1=1.0, scalar2=None, op0=MULT
-        )
+        nc.gpsimd.tensor_scalar(out=cos_f[:], in0=cos_sb[:], scalar1=1.0, scalar2=0.0, op0=MULT, op1=ADD)
+        for e, sign in enumerate((-1.0, 1.0)):
+            nc.gpsimd.tensor_scalar(
+                out=signed_sin_f[:, :, :, e], in0=sin_sb[:], scalar1=sign, scalar2=0.0, op0=MULT, op1=ADD
+            )
 
         w_perm = keep.tile([P, PASSES, 2 * N_OUT], U8, align_bytes=64)
         s_perm = keep.tile([P, PASSES, N_OUT], U8, align_bytes=64)
@@ -135,14 +130,32 @@ def tile_repro_pa_kernel(tc, hidden_states, w_qk_words, w_qk_scales, cos, sin, o
                     in_=w_raw[:, g, :].bitcast(I32).rearrange("p (v i c) -> p i v c", v=VECS, c=2)[:, i0:i1],
                 )
 
-        def reorder_on_gpsimd(stage, mi, by_pair, j0, j1):
-            nc.gpsimd.tensor_scalar(
-                out=stage[:, :, mi, 2 * j0 : 2 * j1].rearrange("p w (j e) -> p w j e", e=2),
-                in0=by_pair[:].rearrange("p j (w e) -> p w j e", e=2),
-                scalar1=1.0,
-                scalar2=0.0,
-                op0=MULT,
-                op1=ADD,
+        def sin_product(rows, x, m, j0, groups):
+            count = x.shape[2]
+            nc.vector.tensor_tensor(
+                out=rows.rearrange("p w (ii jj e) -> p ii w jj e", ii=groups, jj=2),
+                in0=x.rearrange("p ii w (jj e) -> p ii w jj e", jj=2)[:, :, :, :, ::-1],
+                in1=signed_sin_f[:, m, j0 : j0 + 2 * groups, :]
+                .rearrange("p (ii jj) e -> p ii jj e", ii=groups)
+                .unsqueeze(2)
+                .to_broadcast([P, groups, count, 2, 2]),
+                op=MULT,
+            )
+
+        def cos_product(by_cos, x, m, j0, groups):
+            for jl in range(2 * groups):
+                ii, jj = divmod(jl, 2)
+                nc.scalar.activation(
+                    out=by_cos[:, jl, :].rearrange("p (w e) -> p w e", e=2),
+                    in_=x[:, ii, :, 2 * jj : 2 * jj + 2],
+                    func=COPY,
+                    scale=cos_f[:, m, j0 + jl : j0 + jl + 1],
+                )
+
+        def add_cos_product(engine, rows, by_cos):
+            sums = rows.rearrange("p w (j e) -> p w j e", e=2)
+            engine.tensor_tensor(
+                out=sums, in0=sums, in1=by_cos[:].rearrange("p j (w e) -> p w j e", e=2), op=ADD
             )
 
         def project(out, m, b, first, width):
@@ -171,31 +184,39 @@ def tile_repro_pa_kernel(tc, hidden_states, w_qk_words, w_qk_scales, cos, sin, o
                         part = N_GROUP * (B * ii + b)
                         project(acc[:, part : part + N_GROUP], m, b, N_GROUP * (2 * k + ii), N_GROUP)
                 x = acc[:].rearrange("p (ii w c) -> p ii w c", ii=2, c=4)
+                j0 = BANK_PAIRS * k
+                rows = stage[:, :, mi, 2 * j0 : 2 * (j0 + BANK_PAIRS)]
+                if k in GPSIMD_BANKS:
+                    by_cos = cos_pool.tile([P, BANK_PAIRS, 2 * ROWS], F32)
+                    cos_product(by_cos, x, m, j0, 2)
+                    sin_product(rows, x, m, j0, 2)
+                    add_cos_product(nc.gpsimd, rows, by_cos)
+                    continue
                 by_sin = sin_pool.tile([P, BANK_PAIRS, 2, ROWS], F32)
                 by_pair = pair_pool.tile([P, BANK_PAIRS, 2 * ROWS], F32)
                 for jl in range(BANK_PAIRS):
                     ii, jj = divmod(jl, 2)
-                    j = BANK_PAIRS * k + jl
-                    nc.scalar.activation(
-                        out=by_sin[:, jl, 0, :], in_=x[:, ii, :, 2 * jj + 1], func=COPY,
-                        scale=neg_sin_f[:, m, j : j + 1],
-                    )
-                    nc.scalar.activation(
-                        out=by_sin[:, jl, 1, :], in_=x[:, ii, :, 2 * jj], func=COPY,
-                        scale=sin_f[:, m, j : j + 1],
-                    )
+                    for e in range(2):
+                        nc.scalar.activation(
+                            out=by_sin[:, jl, e, :], in_=x[:, ii, :, 2 * jj + 1 - e], func=COPY,
+                            scale=signed_sin_f[:, m, j0 + jl, e : e + 1],
+                        )
                 for jl in range(BANK_PAIRS):
                     ii, jj = divmod(jl, 2)
-                    j = BANK_PAIRS * k + jl
                     nc.vector.scalar_tensor_tensor(
                         out=by_pair[:, jl, :].rearrange("p (w e) -> p w e", e=2),
                         in0=x[:, ii, :, 2 * jj : 2 * jj + 2],
-                        scalar=cos_f[:, m, j : j + 1],
+                        scalar=cos_f[:, m, j0 + jl : j0 + jl + 1],
                         in1=by_sin[:, jl, :, :].rearrange("p e w -> p w e"),
                         op0=MULT,
                         op1=ADD,
                     )
-                reorder_on_gpsimd(stage, mi, by_pair, BANK_PAIRS * k, BANK_PAIRS * (k + 1))
+                dst = rows.rearrange("p w (j e) -> p w j e", e=2)
+                src = by_pair[:].rearrange("p j (w e) -> p w j e", e=2)
+                if k in SCALAR_BANKS:
+                    nc.scalar.copy(out=dst, in_=src)
+                else:
+                    nc.vector.tensor_copy(out=dst, in_=src)
 
         def one_batch(m, b, stage):
             mi = m % M_GROUP
@@ -205,37 +226,18 @@ def tile_repro_pa_kernel(tc, hidden_states, w_qk_words, w_qk_scales, cos, sin, o
                 x = acc[:].rearrange("p (ii v c) -> p ii v c", ii=4, c=4)
                 j0 = B * BANK_PAIRS * k
                 by_cos = cos_pool.tile([P, B * BANK_PAIRS, 2 * VECS], F32)
-                for jl in range(B * BANK_PAIRS):
-                    ii, jj = divmod(jl, 2)
-                    nc.scalar.activation(
-                        out=by_cos[:, jl, :].rearrange("p (v e) -> p v e", e=2),
-                        in_=x[:, ii, :, 2 * jj : 2 * jj + 2],
-                        func=COPY,
-                        scale=cos_f[:, m, j0 + jl : j0 + jl + 1],
-                    )
                 rows = stage[:, VECS * b : VECS * (b + 1), mi, 2 * j0 : 2 * (j0 + B * BANK_PAIRS)]
-                nc.vector.tensor_tensor(
-                    out=rows.rearrange("p v (ii jj e) -> p ii v jj e", ii=4, jj=2),
-                    in0=x.rearrange("p ii v (jj e) -> p ii v jj e", jj=2)[:, :, :, :, ::-1],
-                    in1=signed_sin_f[:, (m - SPLIT_FROM) // 2, j0 : j0 + B * BANK_PAIRS, :]
-                    .rearrange("p (ii jj) e -> p ii jj e", ii=4)
-                    .unsqueeze(2)
-                    .to_broadcast([P, 4, VECS, 2, 2]),
-                    op=MULT,
-                )
-                sums = rows.rearrange("p v (j e) -> p v j e", e=2)
-                last_half = m == M_PER_P - 1 and b == B - 1
-                adder = nc.gpsimd if k % 2 == 0 and not last_half else nc.vector
-                adder.tensor_tensor(
-                    out=sums, in0=sums, in1=by_cos[:].rearrange("p j (v e) -> p v j e", e=2), op=ADD
-                )
+                cos_product(by_cos, x, m, j0, 4)
+                sin_product(rows, x, m, j0, 4)
+                adder = nc.gpsimd if k % 2 == 0 and b == 0 else nc.vector
+                add_cos_product(adder, rows, by_cos)
 
         for m in range(M_PER_P):
             if m + 1 < M_PER_P:
                 quantise_slot(m + 1)
             if m % M_GROUP == 0:
                 stage = stage_pool.tile([P, ROWS, M_GROUP, HEAD_DIM], F32)
-            split = m >= SPLIT_FROM and (m - SPLIT_FROM) % 2 == 0
+            split = m == M_PER_P - 1
             if not split:
                 both_batches(m, stage)
             for b in range(B):

@@ -33,8 +33,9 @@ FLOPS = 2 * S * B * H * N_OUT
 
 M_GROUP = 2
 PERM_CHUNKS = ((0,4),(4,16),)
-GPSIMD_BANKS = (0, 2, 3, 5, 7)
+SPLIT_BANKS = 6
 SCALAR_BANKS = (1, 4)
+BATCH_BEFORE = {2: 0, 5: 1}
 
 
 def tile_repro_pa_kernel(tc, hidden_states, w_qk_words, w_qk_scales, cos, sin, out_0, out_1):
@@ -48,8 +49,8 @@ def tile_repro_pa_kernel(tc, hidden_states, w_qk_words, w_qk_scales, cos, sin, o
         keep = ctx.enter_context(tc.tile_pool(name="keep", bufs=1))
         group_pool = ctx.enter_context(tc.tile_pool(name="grouped", bufs=3))
         sin_pool = ctx.enter_context(tc.tile_pool(name="by_sin", bufs=6))
-        pair_pool = ctx.enter_context(tc.tile_pool(name="by_pair", bufs=4))
-        cos_pool = ctx.enter_context(tc.tile_pool(name="by_cos", bufs=8))
+        pair_pool = ctx.enter_context(tc.tile_pool(name="by_pair", bufs=10))
+        cos_pool = ctx.enter_context(tc.tile_pool(name="by_cos", bufs=6))
         stage_pool = ctx.enter_context(tc.tile_pool(name="stage", bufs=2))
         psum_t = ctx.enter_context(tc.psum_pool(name="psum_t", bufs=2))
         psum_acc = ctx.enter_context(tc.psum_pool(name="psum_acc", bufs=6))
@@ -78,7 +79,7 @@ def tile_repro_pa_kernel(tc, hidden_states, w_qk_words, w_qk_scales, cos, sin, o
         for m in range(1, M_PER_P):
             nc.sync.dma_start(out=x_tiles[m][:], in_=x_dram[:, m, :])
 
-        cos_f = keep.tile([P, M_PER_P, PAIRS], F32)
+        cos_f = keep.tile([P, M_PER_P, PAIRS, 2], F32)
         signed_sin_f = keep.tile([P, M_PER_P, PAIRS, 2], F32)
 
         ident = keep.tile([P, P], F32)
@@ -99,10 +100,7 @@ def tile_repro_pa_kernel(tc, hidden_states, w_qk_words, w_qk_scales, cos, sin, o
                             flipped[:, g, u, :], words[:, first + u : first + K_PASS // 2 : 2], ident[:]
                         )
                 half = grouped[:, b].bitcast(F32)
-                if b == 0:
-                    nc.scalar.copy(out=half, in_=flipped[:].rearrange("p g u r -> p g r u"))
-                else:
-                    nc.vector.tensor_copy(out=half, in_=flipped[:].rearrange("p g u r -> p g r u"))
+                nc.scalar.copy(out=half, in_=flipped[:].rearrange("p g u r -> p g r u"))
             nc.vector.quantize_mx(
                 out=x_codes[:, m].rearrange("p b g r -> p (b g r)").bitcast(FP8X4),
                 scales=x_scales[:, m].rearrange("p b g r -> p (b g r)"),
@@ -111,11 +109,11 @@ def tile_repro_pa_kernel(tc, hidden_states, w_qk_words, w_qk_scales, cos, sin, o
 
         quantise_slot(0)
 
-        nc.gpsimd.tensor_scalar(out=cos_f[:], in0=cos_sb[:], scalar1=1.0, scalar2=0.0, op0=MULT, op1=ADD)
         for e, sign in enumerate((-1.0, 1.0)):
-            nc.gpsimd.tensor_scalar(
-                out=signed_sin_f[:, :, :, e], in0=sin_sb[:], scalar1=sign, scalar2=0.0, op0=MULT, op1=ADD
-            )
+            for table, values, factor in ((cos_f, cos_sb, 1.0), (signed_sin_f, sin_sb, sign)):
+                nc.gpsimd.tensor_scalar(
+                    out=table[:, :, :, e], in0=values[:], scalar1=factor, scalar2=0.0, op0=MULT, op1=ADD
+                )
 
         w_perm = keep.tile([P, PASSES, 2 * N_OUT], U8, align_bytes=64)
         s_perm = keep.tile([P, PASSES, N_OUT], U8, align_bytes=64)
@@ -130,15 +128,19 @@ def tile_repro_pa_kernel(tc, hidden_states, w_qk_words, w_qk_scales, cos, sin, o
                     in_=w_raw[:, g, :].bitcast(I32).rearrange("p (v i c) -> p i v c", v=VECS, c=2)[:, i0:i1],
                 )
 
+        def over_rows(table, m, j0, groups, count):
+            return (
+                table[:, m, j0 : j0 + 2 * groups, :]
+                .rearrange("p (ii jj) e -> p ii jj e", ii=groups)
+                .unsqueeze(2)
+                .to_broadcast([P, groups, count, 2, 2])
+            )
+
         def sin_product(rows, x, m, j0, groups):
-            count = x.shape[2]
             nc.vector.tensor_tensor(
                 out=rows.rearrange("p w (ii jj e) -> p ii w jj e", ii=groups, jj=2),
                 in0=x.rearrange("p ii w (jj e) -> p ii w jj e", jj=2)[:, :, :, :, ::-1],
-                in1=signed_sin_f[:, m, j0 : j0 + 2 * groups, :]
-                .rearrange("p (ii jj) e -> p ii jj e", ii=groups)
-                .unsqueeze(2)
-                .to_broadcast([P, groups, count, 2, 2]),
+                in1=over_rows(signed_sin_f, m, j0, groups, x.shape[2]),
                 op=MULT,
             )
 
@@ -149,14 +151,16 @@ def tile_repro_pa_kernel(tc, hidden_states, w_qk_words, w_qk_scales, cos, sin, o
                     out=by_cos[:, jl, :].rearrange("p (w e) -> p w e", e=2),
                     in_=x[:, ii, :, 2 * jj : 2 * jj + 2],
                     func=COPY,
-                    scale=cos_f[:, m, j0 + jl : j0 + jl + 1],
+                    scale=cos_f[:, m, j0 + jl, 0:1],
                 )
 
-        def add_cos_product(engine, rows, by_cos):
-            sums = rows.rearrange("p w (j e) -> p w j e", e=2)
-            engine.tensor_tensor(
-                out=sums, in0=sums, in1=by_cos[:].rearrange("p j (w e) -> p w j e", e=2), op=ADD
-            )
+        copies = []
+        waiting = []
+
+        def add_waiting():
+            for sums, products in waiting:
+                nc.vector.tensor_tensor(out=sums, in0=sums, in1=products, op=ADD)
+            waiting.clear()
 
         def project(out, m, b, first, width):
             for g in range(PASSES):
@@ -175,73 +179,81 @@ def tile_repro_pa_kernel(tc, hidden_states, w_qk_words, w_qk_scales, cos, sin, o
             for q in range(2):
                 nc.sync.dma_start(out=out_views[q][b, m_set], in_=rows[:, b, :, q, :])
 
-        def both_batches(m, stage):
-            mi = m % M_GROUP
-            for k in range(BANKS):
-                acc = psum_acc.tile([P, 4 * N_GROUP], F32)
-                for ii in range(2):
-                    for b in range(B):
-                        part = N_GROUP * (B * ii + b)
-                        project(acc[:, part : part + N_GROUP], m, b, N_GROUP * (2 * k + ii), N_GROUP)
-                x = acc[:].rearrange("p (ii w c) -> p ii w c", ii=2, c=4)
-                j0 = BANK_PAIRS * k
-                rows = stage[:, :, mi, 2 * j0 : 2 * (j0 + BANK_PAIRS)]
-                if k in GPSIMD_BANKS:
-                    by_cos = cos_pool.tile([P, BANK_PAIRS, 2 * ROWS], F32)
-                    cos_product(by_cos, x, m, j0, 2)
-                    sin_product(rows, x, m, j0, 2)
-                    add_cos_product(nc.gpsimd, rows, by_cos)
-                    continue
-                by_sin = sin_pool.tile([P, BANK_PAIRS, 2, ROWS], F32)
-                by_pair = pair_pool.tile([P, BANK_PAIRS, 2 * ROWS], F32)
-                for jl in range(BANK_PAIRS):
-                    ii, jj = divmod(jl, 2)
-                    for e in range(2):
-                        nc.scalar.activation(
-                            out=by_sin[:, jl, e, :], in_=x[:, ii, :, 2 * jj + 1 - e], func=COPY,
-                            scale=signed_sin_f[:, m, j0 + jl, e : e + 1],
-                        )
-                for jl in range(BANK_PAIRS):
-                    ii, jj = divmod(jl, 2)
-                    nc.vector.scalar_tensor_tensor(
-                        out=by_pair[:, jl, :].rearrange("p (w e) -> p w e", e=2),
-                        in0=x[:, ii, :, 2 * jj : 2 * jj + 2],
-                        scalar=cos_f[:, m, j0 + jl : j0 + jl + 1],
-                        in1=by_sin[:, jl, :, :].rearrange("p e w -> p w e"),
-                        op0=MULT,
-                        op1=ADD,
+        def by_scalars(m, k, stage):
+            acc = psum_acc.tile([P, 4 * N_GROUP], F32)
+            for ii in range(2):
+                for b in range(B):
+                    part = N_GROUP * (B * ii + b)
+                    project(acc[:, part : part + N_GROUP], m, b, N_GROUP * (2 * k + ii), N_GROUP)
+            x = acc[:].rearrange("p (ii w c) -> p ii w c", ii=2, c=4)
+            j0 = BANK_PAIRS * k
+            by_sin = sin_pool.tile([P, BANK_PAIRS, 2, ROWS], F32)
+            by_pair = pair_pool.tile([P, BANK_PAIRS, 2 * ROWS], F32)
+            for jl in range(BANK_PAIRS):
+                ii, jj = divmod(jl, 2)
+                for e in range(2):
+                    nc.scalar.activation(
+                        out=by_sin[:, jl, e, :], in_=x[:, ii, :, 2 * jj + 1 - e], func=COPY,
+                        scale=signed_sin_f[:, m, j0 + jl, e : e + 1],
                     )
-                dst = rows.rearrange("p w (j e) -> p w j e", e=2)
-                src = by_pair[:].rearrange("p j (w e) -> p w j e", e=2)
-                if k in SCALAR_BANKS:
-                    nc.scalar.copy(out=dst, in_=src)
-                else:
-                    nc.vector.tensor_copy(out=dst, in_=src)
+            for jl in range(BANK_PAIRS):
+                ii, jj = divmod(jl, 2)
+                nc.vector.scalar_tensor_tensor(
+                    out=by_pair[:, jl, :].rearrange("p (w e) -> p w e", e=2),
+                    in0=x[:, ii, :, 2 * jj : 2 * jj + 2],
+                    scalar=cos_f[:, m, j0 + jl, 0:1],
+                    in1=by_sin[:, jl, :, :].rearrange("p e w -> p w e"),
+                    op0=MULT,
+                    op1=ADD,
+                )
+            dst = stage[:, :, m % M_GROUP, 2 * j0 : 2 * (j0 + BANK_PAIRS)].rearrange("p w (j e) -> p w j e", e=2)
+            src = by_pair[:].rearrange("p j (w e) -> p w j e", e=2)
+            if k in SCALAR_BANKS:
+                copies.append((dst, src))
+            else:
+                nc.gpsimd.tensor_scalar(out=dst, in0=src, scalar1=1.0, scalar2=0.0, op0=MULT, op1=ADD)
 
-        def one_batch(m, b, stage):
-            mi = m % M_GROUP
-            for k in range(BANKS // B):
-                acc = psum_acc.tile([P, 4 * N_GROUP], F32)
-                project(acc[:], m, b, 4 * N_GROUP * k, 4 * N_GROUP)
-                x = acc[:].rearrange("p (ii v c) -> p ii v c", ii=4, c=4)
-                j0 = B * BANK_PAIRS * k
-                by_cos = cos_pool.tile([P, B * BANK_PAIRS, 2 * VECS], F32)
-                rows = stage[:, VECS * b : VECS * (b + 1), mi, 2 * j0 : 2 * (j0 + B * BANK_PAIRS)]
-                cos_product(by_cos, x, m, j0, 4)
-                sin_product(rows, x, m, j0, 4)
-                adder = nc.gpsimd if k % 2 == 0 and b == 0 else nc.vector
-                add_cos_product(adder, rows, by_cos)
+        def copy_waiting(left):
+            while len(copies) > left:
+                dst, src = copies[0]
+                copies.remove(copies[0])
+                nc.scalar.copy(out=dst, in_=src)
+
+        def by_table(m, b, k, stage, adder):
+            acc = psum_acc.tile([P, 4 * N_GROUP], F32)
+            project(acc[:], m, b, 4 * N_GROUP * k, 4 * N_GROUP)
+            x = acc[:].rearrange("p (ii v c) -> p ii v c", ii=4, c=4)
+            j0 = B * BANK_PAIRS * k
+            by_cos = cos_pool.tile([P, B * BANK_PAIRS, 2 * VECS], F32)
+            rows = stage[:, VECS * b : VECS * (b + 1), m % M_GROUP, 2 * j0 : 2 * (j0 + B * BANK_PAIRS)]
+            cos_product(by_cos, x, m, j0, 4)
+            sin_product(rows, x, m, j0, 4)
+            add_waiting()
+            addition = (
+                rows.rearrange("p v (j e) -> p v j e", e=2),
+                by_cos[:].rearrange("p j (v e) -> p v j e", e=2),
+            )
+            if adder is None:
+                waiting.append(addition)
+            else:
+                adder.tensor_tensor(out=addition[0], in0=addition[0], in1=addition[1], op=ADD)
 
         for m in range(M_PER_P):
             if m + 1 < M_PER_P:
                 quantise_slot(m + 1)
             if m % M_GROUP == 0:
                 stage = stage_pool.tile([P, ROWS, M_GROUP, HEAD_DIM], F32)
-            split = m == M_PER_P - 1
-            if not split:
-                both_batches(m, stage)
+            if m < M_PER_P - 1:
+                for k in range(SPLIT_BANKS):
+                    if k in BATCH_BEFORE:
+                        by_table(m, BATCH_BEFORE[k], SPLIT_BANKS // B, stage, nc.gpsimd)
+                    copy_waiting(1)
+                    by_scalars(m, k, stage)
+                copy_waiting(0)
             for b in range(B):
-                if split:
-                    one_batch(m, b, stage)
+                if m == M_PER_P - 1:
+                    for k in range(BANKS // B):
+                        by_table(m, b, k, stage, None)
+                    add_waiting()
                 if m % M_GROUP == M_GROUP - 1:
                     store(stage, m // M_GROUP, b)

@@ -34,7 +34,6 @@ FLOPS = 2 * S * B * H * N_OUT
 M_GROUP = 2
 PERM_CHUNKS = ((0,4),(4,16),)
 SPLIT_BANKS = 6
-SCALAR_BANKS = (1, 4)
 BATCH_BEFORE = {2: 0, 5: 1}
 
 
@@ -154,7 +153,6 @@ def tile_repro_pa_kernel(tc, hidden_states, w_qk_words, w_qk_scales, cos, sin, o
                     scale=cos_f[:, m, j0 + jl, 0:1],
                 )
 
-        copies = []
         waiting = []
 
         def add_waiting():
@@ -208,18 +206,10 @@ def tile_repro_pa_kernel(tc, hidden_states, w_qk_words, w_qk_scales, cos, sin, o
                 )
             dst = stage[:, :, m % M_GROUP, 2 * j0 : 2 * (j0 + BANK_PAIRS)].rearrange("p w (j e) -> p w j e", e=2)
             src = by_pair[:].rearrange("p j (w e) -> p w j e", e=2)
-            if k in SCALAR_BANKS:
-                copies.append((dst, src))
-            else:
-                nc.gpsimd.tensor_scalar(out=dst, in0=src, scalar1=1.0, scalar2=0.0, op0=MULT, op1=ADD)
+            nc.gpsimd.tensor_scalar(out=dst, in0=src, scalar1=1.0, scalar2=0.0, op0=MULT, op1=ADD)
+            add_waiting()
 
-        def copy_waiting(left):
-            while len(copies) > left:
-                dst, src = copies[0]
-                copies.remove(copies[0])
-                nc.scalar.copy(out=dst, in_=src)
-
-        def by_table(m, b, k, stage, adder):
+        def by_table(m, b, k, stage):
             acc = psum_acc.tile([P, 4 * N_GROUP], F32)
             project(acc[:], m, b, 4 * N_GROUP * k, 4 * N_GROUP)
             x = acc[:].rearrange("p (ii v c) -> p ii v c", ii=4, c=4)
@@ -229,14 +219,12 @@ def tile_repro_pa_kernel(tc, hidden_states, w_qk_words, w_qk_scales, cos, sin, o
             cos_product(by_cos, x, m, j0, 4)
             sin_product(rows, x, m, j0, 4)
             add_waiting()
-            addition = (
-                rows.rearrange("p v (j e) -> p v j e", e=2),
-                by_cos[:].rearrange("p j (v e) -> p v j e", e=2),
+            waiting.append(
+                (
+                    rows.rearrange("p v (j e) -> p v j e", e=2),
+                    by_cos[:].rearrange("p j (v e) -> p v j e", e=2),
+                )
             )
-            if adder is None:
-                waiting.append(addition)
-            else:
-                adder.tensor_tensor(out=addition[0], in0=addition[0], in1=addition[1], op=ADD)
 
         for m in range(M_PER_P):
             if m + 1 < M_PER_P:
@@ -246,14 +234,13 @@ def tile_repro_pa_kernel(tc, hidden_states, w_qk_words, w_qk_scales, cos, sin, o
             if m < M_PER_P - 1:
                 for k in range(SPLIT_BANKS):
                     if k in BATCH_BEFORE:
-                        by_table(m, BATCH_BEFORE[k], SPLIT_BANKS // B, stage, nc.gpsimd)
-                    copy_waiting(1)
+                        b = BATCH_BEFORE[k]
+                        by_table(m, b, SPLIT_BANKS // B, stage)
                     by_scalars(m, k, stage)
-                copy_waiting(0)
             for b in range(B):
                 if m == M_PER_P - 1:
                     for k in range(BANKS // B):
-                        by_table(m, b, k, stage, None)
+                        by_table(m, b, k, stage)
                     add_waiting()
                 if m % M_GROUP == M_GROUP - 1:
                     store(stage, m // M_GROUP, b)

from contextlib import ExitStack

import concourse.mybir as mybir
from concourse.masks import make_identity

F32 = mybir.dt.float32
BF16 = mybir.dt.bfloat16
I32 = mybir.dt.int32
U32 = mybir.dt.uint32
U8 = mybir.dt.uint8
FP8X4 = mybir.dt.float8_e4m3fn_x4
FP4X4 = mybir.dt.float4_e2m1fn_x4
MULT = mybir.AluOpType.mult
ADD = mybir.AluOpType.add
COPY = mybir.ActivationFunctionType.Copy

P = 128
S, B, H = 1024, 2, 1024
HEADS, HEAD_DIM = 16, 64
PAIRS = HEAD_DIM // 2
VECS = 2 * HEADS
N_OUT = VECS * HEAD_DIM
K_PASS = 4 * P
PASSES = H // K_PASS
M_PER_P = S // P
N_GROUP = 128
GROUPS = N_OUT // N_GROUP
ROWS = B * VECS
BANK_PAIRS = 4
BANKS = PAIRS // BANK_PAIRS

FLOPS = 2 * S * B * H * N_OUT

M_GROUP = 2
PERM_CHUNKS = ((0,4),(4,16),)
SPLIT_BANKS = 6
BATCH_BEFORE = {2: 0, 5: 1}


def tile_repro_pa_kernel(tc, hidden_states, w_qk_words, w_qk_scales, cos, sin, out_0, out_1):
    nc = tc.nc
    x_dram = hidden_states.rearrange("(p m) b k -> p m (b k)", m=M_PER_P)
    out_views = [
        o.rearrange("(b h) (p g m) d -> b g p h (m d)", b=B, p=P, m=M_GROUP) for o in (out_0, out_1)
    ]

    with ExitStack() as ctx:
        keep = ctx.enter_context(tc.tile_pool(name="keep", bufs=1))
        group_pool = ctx.enter_context(tc.tile_pool(name="grouped", bufs=3))
        sin_pool = ctx.enter_context(tc.tile_pool(name="by_sin", bufs=6))
        pair_pool = ctx.enter_context(tc.tile_pool(name="by_pair", bufs=10))
        cos_pool = ctx.enter_context(tc.tile_pool(name="by_cos", bufs=6))
        stage_pool = ctx.enter_context(tc.tile_pool(name="stage", bufs=2))
        psum_t = ctx.enter_context(tc.psum_pool(name="psum_t", bufs=2))
        psum_acc = ctx.enter_context(tc.psum_pool(name="psum_acc", bufs=6))

        s_raw = keep.tile([P, PASSES, N_OUT], U8, align_bytes=64)
        nc.vector.memset(s_raw[:].bitcast(I32), 0)
        w_raw = keep.tile([P, PASSES, 2 * N_OUT], U8, align_bytes=64)
        x_tiles = []
        for m in range(M_PER_P):
            x_m = keep.tile([P, B * H], BF16, name="x%d" % m)
            x_tiles.append(x_m)
        nc.sync.dma_start(out=x_tiles[0][:], in_=x_dram[:, 0, :])
        cos_sb = keep.tile([P, M_PER_P, PAIRS], BF16)
        sin_sb = keep.tile([P, M_PER_P, PAIRS], BF16)
        nc.sync.dma_start(out=sin_sb[:], in_=sin.rearrange("(p m) j -> p m j", m=M_PER_P))
        nc.sync.dma_start(out=cos_sb[:], in_=cos.rearrange("(p m) j -> p m j", m=M_PER_P))
        for g in range(PASSES):
            nc.sync.dma_start(out=w_raw[:, g, :].bitcast(I32), in_=w_qk_words[g].bitcast(I32))
        for g in range(PASSES):
            for quad in range(4):
                nc.sync.dma_start(
                    out=s_raw[32 * quad : 32 * quad + 4, g, :].bitcast(I32),
                    in_=w_qk_scales[g, 4 * quad : 4 * quad + 4, :].bitcast(I32),
                )

        for m in range(1, M_PER_P):
            nc.sync.dma_start(out=x_tiles[m][:], in_=x_dram[:, m, :])

        cos_f = keep.tile([P, M_PER_P, PAIRS, 2], F32)
        signed_sin_f = keep.tile([P, M_PER_P, PAIRS, 2], F32)

        ident = keep.tile([P, P], F32)
        make_identity(nc, ident[:])

        x_codes = keep.tile([P, M_PER_P, B, PASSES, P], U32, align_bytes=64)
        x_scales = keep.tile([P, M_PER_P, B, PASSES, P], U8, align_bytes=64)

        def quantise_slot(m):
            words = x_tiles[m][:].bitcast(F32)
            grouped = group_pool.tile([P, B, PASSES, P, 4], BF16, align_bytes=64)
            for b in range(B):
                flipped = psum_t.tile([P, PASSES, 2, P], F32)
                for g in range(PASSES):
                    for u in range(2):
                        first = (H // 2) * b + (K_PASS // 2) * g
                        nc.tensor.transpose(
                            flipped[:, g, u, :], words[:, first + u : first + K_PASS // 2 : 2], ident[:]
                        )
                half = grouped[:, b].bitcast(F32)
                nc.scalar.copy(out=half, in_=flipped[:].rearrange("p g u r -> p g r u"))
            nc.vector.quantize_mx(
                out=x_codes[:, m].rearrange("p b g r -> p (b g r)").bitcast(FP8X4),
                scales=x_scales[:, m].rearrange("p b g r -> p (b g r)"),
                in_=grouped[:].rearrange("p b g r t -> p (b g r t)"),
            )

        quantise_slot(0)

        for e, sign in enumerate((-1.0, 1.0)):
            for table, values, factor in ((cos_f, cos_sb, 1.0), (signed_sin_f, sin_sb, sign)):
                nc.gpsimd.tensor_scalar(
                    out=table[:, :, :, e], in0=values[:], scalar1=factor, scalar2=0.0, op0=MULT, op1=ADD
                )

        w_perm = keep.tile([P, PASSES, 2 * N_OUT], U8, align_bytes=64)
        s_perm = keep.tile([P, PASSES, N_OUT], U8, align_bytes=64)
        for i0, i1 in PERM_CHUNKS:
            for g in range(PASSES):
                nc.vector.tensor_copy(
                    out=s_perm[:, g, :].bitcast(I32).rearrange("p (i v) -> p i v", v=VECS)[:, i0:i1, :],
                    in_=s_raw[:, g, :].bitcast(I32).rearrange("p (v i) -> p i v", v=VECS)[:, i0:i1, :],
                )
                nc.vector.tensor_copy(
                    out=w_perm[:, g, :].bitcast(I32).rearrange("p (i v c) -> p i v c", v=VECS, c=2)[:, i0:i1],
                    in_=w_raw[:, g, :].bitcast(I32).rearrange("p (v i c) -> p i v c", v=VECS, c=2)[:, i0:i1],
                )

        def over_rows(table, m, j0, groups, count):
            return (
                table[:, m, j0 : j0 + 2 * groups, :]
                .rearrange("p (ii jj) e -> p ii jj e", ii=groups)
                .unsqueeze(2)
                .to_broadcast([P, groups, count, 2, 2])
            )

        def sin_product(rows, x, m, j0, groups):
            nc.vector.tensor_tensor(
                out=rows.rearrange("p w (ii jj e) -> p ii w jj e", ii=groups, jj=2),
                in0=x.rearrange("p ii w (jj e) -> p ii w jj e", jj=2)[:, :, :, :, ::-1],
                in1=over_rows(signed_sin_f, m, j0, groups, x.shape[2]),
                op=MULT,
            )

        def cos_product(by_cos, x, m, j0, groups):
            for jl in range(2 * groups):
                ii, jj = divmod(jl, 2)
                nc.scalar.activation(
                    out=by_cos[:, jl, :].rearrange("p (w e) -> p w e", e=2),
                    in_=x[:, ii, :, 2 * jj : 2 * jj + 2],
                    func=COPY,
                    scale=cos_f[:, m, j0 + jl, 0:1],
                )

        waiting = []

        def add_waiting():
            for sums, products in waiting:
                nc.vector.tensor_tensor(out=sums, in0=sums, in1=products, op=ADD)
            waiting.clear()

        def project(out, m, b, first, width):
            for g in range(PASSES):
                nc.tensor.matmul_mx(
                    out=out,
                    lhsT=x_codes[:, m, b, g, :].bitcast(FP8X4),
                    lhsT_scale=x_scales[:, m, b, g, :],
                    rhs=w_perm[:, g, 2 * first : 2 * (first + width)].bitcast(FP4X4),
                    rhs_scale=s_perm[:, g, first : first + width],
                    start=(g == 0),
                    stop=(g == PASSES - 1),
                )

        def store(stage, m_set, b):
            rows = stage[:].rearrange("p (b h q) m d -> p b h q (m d)", b=B, q=2)
            for q in range(2):
                nc.sync.dma_start(out=out_views[q][b, m_set], in_=rows[:, b, :, q, :])

        def by_scalars(m, k, stage):
            acc = psum_acc.tile([P, 4 * N_GROUP], F32)
            for ii in range(2):
                for b in range(B):
                    part = N_GROUP * (B * ii + b)
                    project(acc[:, part : part + N_GROUP], m, b, N_GROUP * (2 * k + ii), N_GROUP)
            x = acc[:].rearrange("p (ii w c) -> p ii w c", ii=2, c=4)
            j0 = BANK_PAIRS * k
            by_sin = sin_pool.tile([P, BANK_PAIRS, 2, ROWS], F32)
            by_pair = pair_pool.tile([P, BANK_PAIRS, 2 * ROWS], F32)
            for jl in range(BANK_PAIRS):
                ii, jj = divmod(jl, 2)
                for e in range(2):
                    nc.scalar.activation(
                        out=by_sin[:, jl, e, :], in_=x[:, ii, :, 2 * jj + 1 - e], func=COPY,
                        scale=signed_sin_f[:, m, j0 + jl, e : e + 1],
                    )
            for jl in range(BANK_PAIRS):
                ii, jj = divmod(jl, 2)
                nc.vector.scalar_tensor_tensor(
                    out=by_pair[:, jl, :].rearrange("p (w e) -> p w e", e=2),
                    in0=x[:, ii, :, 2 * jj : 2 * jj + 2],
                    scalar=cos_f[:, m, j0 + jl, 0:1],
                    in1=by_sin[:, jl, :, :].rearrange("p e w -> p w e"),
                    op0=MULT,
                    op1=ADD,
                )
            dst = stage[:, :, m % M_GROUP, 2 * j0 : 2 * (j0 + BANK_PAIRS)].rearrange("p w (j e) -> p w j e", e=2)
            src = by_pair[:].rearrange("p j (w e) -> p w j e", e=2)
            nc.gpsimd.tensor_scalar(out=dst, in0=src, scalar1=1.0, scalar2=0.0, op0=MULT, op1=ADD)
            add_waiting()

        def by_table(m, b, k, stage):
            acc = psum_acc.tile([P, 4 * N_GROUP], F32)
            project(acc[:], m, b, 4 * N_GROUP * k, 4 * N_GROUP)
            x = acc[:].rearrange("p (ii v c) -> p ii v c", ii=4, c=4)
            j0 = B * BANK_PAIRS * k
            by_cos = cos_pool.tile([P, B * BANK_PAIRS, 2 * VECS], F32)
            rows = stage[:, VECS * b : VECS * (b + 1), m % M_GROUP, 2 * j0 : 2 * (j0 + B * BANK_PAIRS)]
            cos_product(by_cos, x, m, j0, 4)
            sin_product(rows, x, m, j0, 4)
            add_waiting()
            waiting.append(
                (
                    rows.rearrange("p v (j e) -> p v j e", e=2),
                    by_cos[:].rearrange("p j (v e) -> p v j e", e=2),
                )
            )

        for m in range(M_PER_P):
            if m + 1 < M_PER_P:
                quantise_slot(m + 1)
            if m % M_GROUP == 0:
                stage = stage_pool.tile([P, ROWS, M_GROUP, HEAD_DIM], F32)
            if m < M_PER_P - 1:
                for k in range(SPLIT_BANKS):
                    if k in BATCH_BEFORE:
                        b = BATCH_BEFORE[k]
                        by_table(m, b, SPLIT_BANKS // B, stage)
                    by_scalars(m, k, stage)
            for b in range(B):
                if m == M_PER_P - 1:
                    for k in range(BANKS // B):
                        by_table(m, b, k, stage)
                    add_waiting()
                if m % M_GROUP == M_GROUP - 1:
                    store(stage, m // M_GROUP, b)
